import numpy as np
import ml_dtypes


def mxq(x, axis, fmt="e4m3"):
    dtype, down = {"e4m3": (ml_dtypes.float8_e4m3fn, 7), "e5m2": (ml_dtypes.float8_e5m2, 14)}[fmt]
    v = np.moveaxis(np.asarray(x, np.float32).astype(ml_dtypes.bfloat16).astype(np.float64), axis, -1)
    blocks = v.reshape(v.shape[:-1] + (-1, 32))
    amax = np.abs(blocks).max(-1, keepdims=True)
    byte = np.maximum(np.where(amax > 0, np.frexp(amax)[1] - 1 + 127, 0) - down, 1)
    scale = np.exp2(byte - 127.0)
    codes = (blocks / scale).astype(np.float32).astype(dtype).astype(np.float64)
    return np.moveaxis((codes * scale).reshape(v.shape), -1, axis)


WIDE = False


def mx_kscale(k):
    if not WIDE:
        return np.ones(k)
    levels = np.array([10, -10, 5, -5, 0])
    if k % 512:
        return np.exp2(np.random.permutation(np.resize(levels, k // 32))).repeat(32)
    a = np.empty((k // 512, 16))
    for p in range(k // 512):
        a[p, :8] = np.random.permutation(np.resize(levels, 8))
        for g in range(8):
            far = levels[np.abs(levels - a[p, g]) >= 10]
            a[p, g + 8] = far[np.random.randint(len(far))]
    return np.exp2(a.ravel()).repeat(32)


BF16 = ml_dtypes.bfloat16


def bf(x):
    return np.asarray(x, np.float32).astype(BF16)


def f64(x):
    return np.asarray(x).astype(np.float64)


BATCH, ROWS, COLS, IN_DIM, OUT_DIM = 2, 64, 64, 512, 512
N = ROWS * COLS
EPS_BN = 1e-5
EPS_DEG = 1e-5


def _stencil9(x):
    R, C = x.shape[-3], x.shape[-2]
    pad = [(0, 0)] * (x.ndim - 3) + [(1, 1), (1, 1), (0, 0)]
    xp = np.pad(x, pad)
    out = np.zeros_like(x)
    for di in range(3):
        for dj in range(3):
            out = out + xp[..., di:di + R, dj:dj + C, :]
    return out


def _deg_inv_sqrt(rows, cols):
    D = _stencil9(np.ones((rows, cols, 1)))[..., 0]
    return (D + EPS_DEG) ** -0.5


def draw0():
    s = mx_kscale(IN_DIM)
    mu = 0.5 * np.random.standard_normal(IN_DIM)
    bound = np.sqrt(6.0 / IN_DIM)
    return {"H": bf((np.random.standard_normal((BATCH, N, IN_DIM)) + mu) * s),
            "W": bf(np.random.uniform(-bound, bound, (IN_DIM, OUT_DIM)) / s[:, None]),
            "gamma": bf(1.0 + 0.1 * np.random.standard_normal(OUT_DIM)),
            "beta": bf(0.2 * np.random.standard_normal(OUT_DIM))}


def core(H, W, gamma, beta):
    B, n_nodes, _ = H.shape
    Ht = mxq(f64(H), 2, "e4m3") @ mxq(f64(W), 0, "e4m3")
    mean = Ht.mean(axis=(0, 1))
    var = Ht.var(axis=(0, 1))
    Ht = (Ht - mean) * (1.0 / np.sqrt(var + EPS_BN)) * f64(gamma) + f64(beta)
    Ht = np.maximum(Ht, 0.0)
    d = _deg_inv_sqrt(ROWS, COLS)[None, :, :, None]
    Hg = Ht.reshape(B, ROWS, COLS, OUT_DIM)
    Hagg = d * _stencil9(Hg * d)
    return Hagg.reshape(B, n_nodes, OUT_DIM)


def e4m3fn_bytes(y):
    return np.clip(np.asarray(y, np.float64), -448.0, 448.0).astype(np.float32).astype(ml_dtypes.float8_e4m3fn).view(np.uint8)


def e4m3fn_values(b):
    return np.asarray(b, np.uint8).view(ml_dtypes.float8_e4m3fn).astype(np.float64)


def setup_inputs():
    d = draw0()
    x0 = np.asarray(d['H']).astype(np.float64)
    s = (np.max(np.abs(x0), axis=(0, 1), keepdims=True) / 448.0).astype(np.float32)
    out = {}
    for k, v in d.items():
        if k == 'H':
            out['H_bytes'] = e4m3fn_bytes(x0 / s.astype(np.float64))
            out['H_scale'] = s
        else:
            out[k] = v
    return out


def reference(H_bytes, H_scale, W, gamma, beta):
    return core(e4m3fn_values(H_bytes) * H_scale.astype(np.float64), W, gamma, beta)

@@ -1,0 +1,379 @@
+from contextlib import ExitStack
+
+import concourse.mybir as mybir
+from concourse.masks import make_identity
+
+F32 = mybir.dt.float32
+BF16 = mybir.dt.bfloat16
+U32 = mybir.dt.uint32
+U8 = mybir.dt.uint8
+FP8 = mybir.dt.float8_e4m3fn
+FP8X4 = mybir.dt.float8_e4m3fn_x4
+ALU = mybir.AluOpType
+ACT = mybir.ActivationFunctionType
+AX = mybir.AxisListType
+
+P = 128
+BATCH, ROWS, COLS, K, NF = 2, 64, 64, 512, 512
+NODES = BATCH * ROWS * COLS
+FC = NF // P
+CB = 4
+NB = COLS // CB
+HALF = P // 2
+HP = HALF + 4
+NPL = FC * CB * HP
+ZW = 2 * NPL + 12
+NZ = 4
+EPS_BN = 1e-5
+D9 = (9.0 + 1e-5) ** -0.5
+D6 = (6.0 + 1e-5) ** -0.5
+D4 = (4.0 + 1e-5) ** -0.5
+RHO = D6 / D9
+KAPPA = (D4 / D9) / (RHO * RHO)
+
+FLOPS = 2 * NODES * K * NF
+
+
+def tile_graphconvolutionbatch_kernel(tc, H_bytes, H_scale, W, gamma, beta, out):
+    nc = tc.nc
+    with ExitStack() as ctx:
+        keep = ctx.enter_context(tc.tile_pool(name="keep", bufs=1))
+        py = ctx.enter_context(tc.psum_pool(name="py", bufs=4))
+        pt = ctx.enter_context(tc.psum_pool(name="pt", bufs=3))
+        pm = ctx.enter_context(tc.psum_pool(name="pm", bufs=1))
+        ctx.enter_context(tc.manual_schedule())
+        ident = keep.tile([P, P], F32)
+        perm = keep.tile([P, P], F32)
+        w_codes = keep.tile([P, NF], U32, align_bytes=64)
+        w_sc = keep.tile([P, NF], U8, align_bytes=64)
+        codes = keep.tile([P, NODES], U32, align_bytes=64)
+        hsc = keep.tile([P, NODES], U8, align_bytes=64)
+        ssq = keep.tile([P, FC, NB], F32)
+        a9 = keep.tile([P, FC], F32)
+        b9 = keep.tile([P, FC], F32)
+        dcol = keep.tile([P, 2], F32)
+        z_bufs = []
+        for i in range(NZ):
+            zb = keep.tile([P, ZW], F32, name="z_buf%d" % i)
+            z_bufs.append(zb)
+
+        def mx_features(y, f, n0):
+            nc.tensor.matmul_mx(
+                out=y[:],
+                lhsT=w_codes[:, f * P : (f + 1) * P].bitcast(FP8X4),
+                lhsT_scale=w_sc[:, f * P : (f + 1) * P],
+                rhs=codes[:, n0 : n0 + 512].bitcast(FP8X4),
+                rhs_scale=hsc[:, n0 : n0 + 512],
+                start=True,
+                stop=True,
+            )
+
+        with ExitStack() as p1:
+            one = p1.enter_context(tc.tile_pool(name="one", bufs=1))
+            hbp = p1.enter_context(tc.tile_pool(name="hbp", bufs=NB))
+            hwp = p1.enter_context(tc.tile_pool(name="hwp", bufs=3))
+            gp = p1.enter_context(tc.tile_pool(name="gp", bufs=3))
+            jp = p1.enter_context(tc.tile_pool(name="jp", bufs=2))
+
+            sb4 = one.tile([P, 4 * K], F32)
+            nc.sync.dma_start(out=sb4[:, 0:K], in_=H_scale.rearrange("a b k -> (a b k)").partition_broadcast(P))
+            hv = H_bytes.rearrange("b (r c) k -> (b r) (c k)", c=COLS)
+            h_bytes_sb = []
+            w_raw = one.tile([P, 4, NF], BF16)
+            for j in range(NB):
+                hb = hbp.tile([P, CB * K], U8, name="h_bytes_tile")
+                nc.sync.dma_start(out=hb[:], in_=hv[:, j * CB * K : (j + 1) * CB * K])
+                h_bytes_sb.append(hb)
+                if j == 0:
+                    nc.sync.dma_start(out=w_raw[:], in_=W.rearrange("(p j) n -> p j n", j=4))
+            gam_bf = one.tile([P, FC], BF16)
+            bet_bf = one.tile([P, FC], BF16)
+            with nc.allow_non_contiguous_dma(reason="512 values, one to a partition and chunk"):
+                nc.sync.dma_start(out=gam_bf[:], in_=gamma.rearrange("(c p) -> p c", p=P))
+                nc.sync.dma_start(out=bet_bf[:], in_=beta.rearrange("(c p) -> p c", p=P))
+
+            make_identity(nc, ident[:])
+            for s in range(2):
+                nc.vector.tensor_copy(
+                    out=perm[:, s * HALF : (s + 1) * HALF].rearrange("p (i b) -> p b i", b=BATCH),
+                    in_=ident[:].rearrange("p (b i t) -> p b i t", b=BATCH, t=2)[:, :, :, 1 - s],
+                )
+            w_grp = one.tile([P, NF, 4], BF16, align_bytes=64)
+            nc.scalar.copy(out=w_grp[:], in_=w_raw[:].rearrange("p j n -> p n j"))
+            for zb in z_bufs:
+                nc.gpsimd.memset(zb[:, 0:4], 0.0)
+                nc.gpsimd.memset(zb[:, 4 : 4 + 2 * NPL].rearrange("p (m x) -> p m x", x=HP)[:, :, HALF:HP], 0.0)
+                nc.gpsimd.memset(zb[:, 4 + 2 * NPL : ZW], 0.0)
+            mhalf = one.tile([P, FC], F32)
+            nc.gpsimd.memset(mhalf[:], -0.5)
+            g9 = one.tile([P, FC], F32)
+            bet9 = one.tile([P, FC], F32)
+            edge = one.tile([P, 1], F32)
+
+            colsum = pm.tile([P, NF], F32, name="colsum")
+            widened = {}
+            grouped = {}
+
+            def small_constants():
+                nc.vector.tensor_scalar(out=g9[:], in0=gam_bf[:], scalar1=D9, scalar2=None, op0=ALU.mult)
+                nc.vector.tensor_scalar(out=bet9[:], in0=bet_bf[:], scalar1=D9, scalar2=None, op0=ALU.mult)
+                nc.vector.tensor_reduce(
+                    out=edge[:],
+                    in_=ident[:].rearrange("p (g w) -> p g w", w=2)[:, 0 : HALF : HALF - 1, :],
+                    axis=AX.XY,
+                    op=ALU.add,
+                )
+                nc.vector.tensor_scalar(
+                    out=dcol[:, 0:1], in0=edge[:], scalar1=D6 - D9, scalar2=D9, op0=ALU.mult, op1=ALU.add
+                )
+                nc.vector.tensor_scalar(
+                    out=dcol[:, 1:2], in0=edge[:], scalar1=D4 - D6, scalar2=D6, op0=ALU.mult, op1=ALU.add
+                )
+
+            def widen(j):
+                hw = hwp.tile([P, CB * K], BF16, name="hw")
+                hb = h_bytes_sb[j]
+                if j == 0:
+                    for cl in range(CB):
+                        cols = slice(cl * K, (cl + 1) * K)
+                        nc.vector.tensor_tensor(
+                            out=hw[:, cols], in0=hb[:, cols].bitcast(FP8), in1=sb4[:, 0:K], op=ALU.mult
+                        )
+                    nc.vector.tensor_copy(out=sb4[:, K : 2 * K], in_=sb4[:, 0:K])
+                    nc.vector.tensor_copy(out=sb4[:, 2 * K : 4 * K], in_=sb4[:, 0 : 2 * K])
+                else:
+                    nc.vector.tensor_tensor(out=hw[:], in0=hb[:].bitcast(FP8), in1=sb4[:], op=ALU.mult)
+                widened[j] = hw
+
+            def turn_in(j):
+                words = widened[j][:].bitcast(F32)
+                g = gp.tile([P, CB * K], BF16, align_bytes=64, name="g")
+                gw = g[:].bitcast(F32)
+                for q in range(CB // 2):
+                    xt = pt.tile([P, 2, 2, P], F32, name="turned")
+                    for cc in range(2):
+                        cl = 2 * q + cc
+                        for u in range(2):
+                            nc.tensor.transpose(
+                                xt[:, cc, u, :], words[:, cl * (K // 2) + u : (cl + 1) * (K // 2) : 2], perm[:]
+                            )
+                    nc.scalar.copy(
+                        out=gw[:, q * K : (q + 1) * K].rearrange("p (c r u) -> p c r u", c=2, u=2),
+                        in_=xt[:].rearrange("p c u r -> p c r u"),
+                    )
+                grouped[j] = g
+
+            def quantise(j):
+                cols = slice(j * CB * P, (j + 1) * CB * P)
+                nc.vector.quantize_mx(out=codes[:, cols].bitcast(FP8X4), scales=hsc[:, cols], in_=grouped[j][:])
+
+            def column_sum(c):
+                nc.tensor.matmul_mx(
+                    out=colsum[:],
+                    lhsT=codes[:, c * P : (c + 1) * P].bitcast(FP8X4),
+                    lhsT_scale=hsc[:, c * P : (c + 1) * P],
+                    rhs=w_codes[:].bitcast(FP8X4),
+                    rhs_scale=w_sc[:],
+                    start=(c == 0),
+                    stop=(c == COLS - 1),
+                )
+
+            def square(j, f):
+                y = py.tile([P, 512], F32, name="y")
+                mx_features(y, f, j * 512)
+                junk = jp.tile([P, 512], BF16, name="junk")
+                nc.scalar.activation(out=junk[:], in_=y[:], func=ACT.Square, accum_out=ssq[:, f, j : j + 1])
+
+            for s in range(NB + 2):
+                if s < NB:
+                    widen(s)
+                    turn_in(s)
+                if s == 1:
+                    nc.vector.quantize_mx(
+                        out=w_codes[:].bitcast(FP8X4), scales=w_sc[:], in_=w_grp[:].rearrange("p n j -> p (n j)")
+                    )
+                if 1 <= s <= NB:
+                    quantise(s - 1)
+                if s == 5:
+                    small_constants()
+                if s >= 2:
+                    j = s - 2
+                    if j == NB - 1:
+                        for cl in range(CB):
+                            column_sum(j * CB + cl)
+                        for f in range(FC):
+                            square(j, f)
+                    else:
+                        square(j, 0)
+                        square(j, 1)
+                        column_sum(j * CB)
+                        column_sum(j * CB + 1)
+                        square(j, 2)
+                        column_sum(j * CB + 2)
+                        square(j, 3)
+                        column_sum(j * CB + 3)
+
+            cs_sb = one.tile([P, NF], F32)
+            nc.vector.tensor_copy(out=cs_sb[:], in_=colsum[:])
+            cst = pt.tile([P, FC, P], F32, name="turned")
+            for f in range(FC):
+                nc.tensor.transpose(cst[:, f, :], cs_sb[:, f * P : (f + 1) * P], ident[:])
+            sum4 = one.tile([P, FC], F32)
+            nc.vector.tensor_reduce(out=sum4[:], in_=cst[:], axis=AX.X, op=ALU.add)
+            nmean = one.tile([P, FC], F32)
+            nc.vector.tensor_scalar(out=nmean[:], in0=sum4[:], scalar1=-1.0 / NODES, scalar2=None, op0=ALU.mult)
+            m2 = one.tile([P, FC], F32)
+            nc.vector.tensor_tensor(out=m2[:], in0=nmean[:], in1=nmean[:], op=ALU.mult)
+            gm = one.tile([P, FC], F32)
+            nc.vector.tensor_tensor(out=gm[:], in0=nmean[:], in1=g9[:], op=ALU.mult)
+            ssq4 = one.tile([P, FC], F32)
+            nc.vector.tensor_reduce(out=ssq4[:], in_=ssq[:], axis=AX.X, op=ALU.add)
+            var = one.tile([P, FC], F32)
+            nc.vector.scalar_tensor_tensor(
+                out=var[:], in0=ssq4[:], scalar=1.0 / NODES, in1=m2[:], op0=ALU.mult, op1=ALU.subtract
+            )
+            ve = one.tile([P, FC], F32)
+            nc.vector.tensor_scalar(out=ve[:], in0=var[:], scalar1=0.0, scalar2=EPS_BN, op0=ALU.max, op1=ALU.add)
+            rstd = one.tile([P, FC], F32)
+            nc.gpsimd.tensor_tensor(out=rstd[:], in0=ve[:], in1=mhalf[:], op=ALU.pow)
+            nc.vector.tensor_tensor(out=a9[:], in0=g9[:], in1=rstd[:], op=ALU.mult)
+            ma = one.tile([P, FC], F32)
+            nc.vector.tensor_tensor(out=ma[:], in0=gm[:], in1=rstd[:], op=ALU.mult)
+            nc.vector.tensor_tensor(out=b9[:], in0=bet9[:], in1=ma[:], op=ALU.add)
+
+        with ExitStack() as p2:
+            up = p2.enter_context(tc.tile_pool(name="up", bufs=2))
+            tvp = p2.enter_context(tc.tile_pool(name="tvp", bufs=5))
+            ucp = p2.enter_context(tc.tile_pool(name="ucp", bufs=4))
+            obp = p2.enter_context(tc.tile_pool(name="obp", bufs=3))
+
+            tv_tiles = {}
+            uc_tiles = {}
+            spare = pm.tile([P, NF], F32, name="colsum")
+
+            def norm_relu(j, f):
+                zb = z_bufs[j % NZ]
+                y = py.tile([P, 512], F32, name="y")
+                mx_features(y, f, j * 512)
+                nc.scalar.activation(
+                    out=zb[:, 4 : 4 + 2 * NPL].rearrange("p (s n x) -> p n s x", s=2, x=HP)[
+                        :, f * CB : (f + 1) * CB, :, 0:HALF
+                    ],
+                    in_=y[:].rearrange("p (c s x) -> p c s x", c=CB, s=2),
+                    func=ACT.Relu,
+                    bias=b9[:, f : f + 1],
+                    scale=a9[:, f : f + 1],
+                )
+
+            def border_weights(j):
+                zb = z_bufs[j % NZ]
+                odd = zb[:, 4 : 4 + NPL]
+                even = zb[:, 4 + NPL : 4 + 2 * NPL]
+                top = even.rearrange("p (n x) -> p n x", x=HP)[:, :, 0:2]
+                bottom = odd.rearrange("p (n x) -> p n x", x=HP)[:, :, HALF - 2 : HALF]
+                nc.vector.tensor_scalar(out=top, in0=top, scalar1=RHO, scalar2=None, op0=ALU.mult)
+                nc.vector.tensor_scalar(out=bottom, in0=bottom, scalar1=RHO, scalar2=None, op0=ALU.mult)
+                if j == 0 or j == NB - 1:
+                    cl = 0 if j == 0 else CB - 1
+                    side = zb[:, 4 : 4 + 2 * NPL].rearrange("p (s f c x) -> p s f c x", s=2, f=FC, c=CB)[
+                        :, :, :, cl, 0:HALF
+                    ]
+                    nc.vector.tensor_scalar(out=side, in0=side, scalar1=RHO, scalar2=None, op0=ALU.mult)
+                    ctop = even.rearrange("p (f c x) -> p f c x", f=FC, c=CB)[:, :, cl, 0:2]
+                    cbot = odd.rearrange("p (f c x) -> p f c x", f=FC, c=CB)[:, :, cl, HALF - 2 : HALF]
+                    nc.vector.tensor_scalar(out=ctop, in0=ctop, scalar1=KAPPA, scalar2=None, op0=ALU.mult)
+                    nc.vector.tensor_scalar(out=cbot, in0=cbot, scalar1=KAPPA, scalar2=None, op0=ALU.mult)
+
+            def row_sums(j):
+                zb = z_bufs[j % NZ]
+                u = up.tile([P, NPL], F32, name="u")
+                tv = tvp.tile([P, 2 * NPL], F32, name="tv")
+                tv_tiles[j] = tv
+                hn = NPL // 2
+                for h in range(2):
+                    nc.vector.tensor_tensor(
+                        out=u[:, h * hn : (h + 1) * hn],
+                        in0=zb[:, 4 + NPL + h * hn : 4 + NPL + (h + 1) * hn],
+                        in1=zb[:, 4 + h * hn : 4 + (h + 1) * hn],
+                        op=ALU.add,
+                    )
+                hq = NPL // 4
+                for h in range(2):
+                    nc.vector.tensor_tensor(
+                        out=tv[:, h * NPL : (h + 1) * NPL].rearrange("p (q e b) -> p q e b", e=2, b=BATCH),
+                        in0=u[:, h * hn : (h + 1) * hn]
+                        .rearrange("p (q b) -> p q b", b=BATCH)
+                        .unsqueeze(2)
+                        .to_broadcast([P, hq, 2, BATCH]),
+                        in1=zb[:, 2 : 2 + 2 * (NPL + 4)].rearrange("p (s q b) -> p q s b", s=2, b=BATCH)[
+                            :, h * hq : (h + 1) * hq, :, :
+                        ],
+                        op=ALU.add,
+                    )
+
+            def column_pairs(j):
+                uc = ucp.tile([P, FC * (CB // 2) * P], F32, name="uc")
+                uc_tiles[j] = uc
+                tvq = tv_tiles[j][:].rearrange("p (n e x) -> p n e x", e=2, x=2 * HP)
+                ucq = uc[:].rearrange("p (n m) -> p n m", m=P)
+                hn = FC * (CB // 2) // 2
+                for h in range(2):
+                    ns = slice(h * hn, (h + 1) * hn)
+                    nc.vector.tensor_tensor(out=ucq[:, ns, :], in0=tvq[:, ns, 0, 0:P], in1=tvq[:, ns, 1, 0:P], op=ALU.add)
+
+            def turn_out(ob, i, c):
+                o = pt.tile([P, NF], F32, name="turned")
+                cn = c - 1 if c % 2 == 0 else c + 1
+                for f in range(FC):
+                    n_uc = f * (CB // 2) + (c % CB) // 2
+                    wins = [uc_tiles[c // CB][:, n_uc * P : (n_uc + 1) * P]]
+                    if 0 <= cn < COLS:
+                        n_tv = f * CB + cn % CB
+                        wins.append(tv_tiles[cn // CB][:, n_tv * 2 * HP : n_tv * 2 * HP + P])
+                    for w in range(len(wins)):
+                        nc.tensor.matmul(
+                            out=o[:, f * P : (f + 1) * P],
+                            lhsT=wins[w],
+                            rhs=ident[:],
+                            is_transpose=True,
+                            start=(w == 0),
+                            stop=(w == len(wins) - 1),
+                        )
+                dsel = 1 if (c == 0 or c == COLS - 1) else 0
+                nc.scalar.activation(out=ob[:, i, :], in_=o[:], func=ACT.Copy, scale=dcol[:, dsel : dsel + 1])
+
+            def store(ob, c0, n):
+                for b in range(BATCH):
+                    nc.sync.dma_start(
+                        out=out[b].rearrange("(r c) f -> r c f", c=COLS)[:, c0 : c0 + n, :], in_=ob[b:P:BATCH, 0:n, :]
+                    )
+
+            for f in range(FC):
+                norm_relu(0, f)
+            for j in range(NB + 2):
+                if 1 <= j <= NB:
+                    border_weights(j - 1)
+                if 2 <= j <= NB + 1:
+                    column_pairs(j - 2)
+                if 1 <= j <= NB:
+                    row_sums(j - 1)
+                grp = j - 2
+                cs = []
+                if grp >= 0:
+                    cs = list(range(max(CB * grp - 1, 0), COLS if grp == NB - 1 else CB * grp + CB - 1))
+                ob = None
+                if cs:
+                    ob = obp.tile([P, CB + 1, NF], F32, name="ob")
+                for h in range(2):
+                    if j + 1 < NB:
+                        norm_relu(j + 1, 2 * h)
+                        norm_relu(j + 1, 2 * h + 1)
+                    lo = (len(cs) + 1) // 2
+                    part = cs[:lo] if h == 0 else cs[lo:]
+                    if part:
+                        for i in range(1 if j + 1 < NB else 2):
+                            mx_features(spare, i, 0)
+                    for c in part:
+                        turn_out(ob, c - cs[0], c)
+                if cs:
+                    store(ob, cs[0], len(cs))

@@ -249,7 +249,6 @@ def tile_graphconvolutionbatch_kernel(tc, H_bytes, H_scale, W, gamma, beta, out)
 
             tv_tiles = {}
             uc_tiles = {}
-            spare = pm.tile([P, NF], F32, name="colsum")
 
             def norm_relu(j, f):
                 zb = z_bufs[j % NZ]
@@ -370,9 +369,6 @@ def tile_graphconvolutionbatch_kernel(tc, H_bytes, H_scale, W, gamma, beta, out)
                         norm_relu(j + 1, 2 * h + 1)
                     lo = (len(cs) + 1) // 2
                     part = cs[:lo] if h == 0 else cs[lo:]
-                    if part:
-                        for i in range(1 if j + 1 < NB else 2):
-                            mx_features(spare, i, 0)
                     for c in part:
                         turn_out(ob, c - cs[0], c)
                 if cs:

@@ -98,6 +98,8 @@ def tile_graphconvolutionbatch_kernel(tc, H_bytes, H_scale, W, gamma, beta, out)
                     out=perm[:, s * HALF : (s + 1) * HALF].rearrange("p (i b) -> p b i", b=BATCH),
                     in_=ident[:].rearrange("p (b i t) -> p b i t", b=BATCH, t=2)[:, :, :, 1 - s],
                 )
+            nc.scalar.copy(out=sb4[:, K : 2 * K], in_=sb4[:, 0:K])
+            nc.scalar.copy(out=sb4[:, 2 * K : 4 * K], in_=sb4[:, 0 : 2 * K])
             w_grp = one.tile([P, NF, 4], BF16, align_bytes=64)
             nc.scalar.copy(out=w_grp[:], in_=w_raw[:].rearrange("p j n -> p n j"))
             for zb in z_bufs:
@@ -139,8 +141,6 @@ def tile_graphconvolutionbatch_kernel(tc, H_bytes, H_scale, W, gamma, beta, out)
                         nc.vector.tensor_tensor(
                             out=hw[:, cols], in0=hb[:, cols].bitcast(FP8), in1=sb4[:, 0:K], op=ALU.mult
                         )
-                    nc.vector.tensor_copy(out=sb4[:, K : 2 * K], in_=sb4[:, 0:K])
-                    nc.vector.tensor_copy(out=sb4[:, 2 * K : 4 * K], in_=sb4[:, 0 : 2 * K])
                 else:
                     nc.vector.tensor_tensor(out=hw[:], in0=hb[:].bitcast(FP8), in1=sb4[:], op=ALU.mult)
                 widened[j] = hw
@@ -184,7 +184,7 @@ def tile_graphconvolutionbatch_kernel(tc, H_bytes, H_scale, W, gamma, beta, out)
                 junk = jp.tile([P, 512], BF16, name="junk")
                 nc.scalar.activation(out=junk[:], in_=y[:], func=ACT.Square, accum_out=ssq[:, f, j : j + 1])
 
-            for s in range(NB + 2):
+            for s in range(NB + 1):
                 if s < NB:
                     widen(s)
                     turn_in(s)
@@ -192,12 +192,12 @@ def tile_graphconvolutionbatch_kernel(tc, H_bytes, H_scale, W, gamma, beta, out)
                     nc.vector.quantize_mx(
                         out=w_codes[:].bitcast(FP8X4), scales=w_sc[:], in_=w_grp[:].rearrange("p n j -> p (n j)")
                     )
-                if 1 <= s <= NB:
+                if s >= 1:
                     quantise(s - 1)
                 if s == 5:
                     small_constants()
-                if s >= 2:
-                    j = s - 2
+                if s >= 1:
+                    j = s - 1
                     if j == NB - 1:
                         for cl in range(CB):
                             column_sum(j * CB + cl)
@@ -317,7 +317,7 @@ def tile_graphconvolutionbatch_kernel(tc, H_bytes, H_scale, W, gamma, beta, out)
                 ucq = uc[:].rearrange("p (n m) -> p n m", m=P)
                 hn = FC * (CB // 2) // 2
                 for h in range(2):
-                    ns = slice(h * hn, (h + 1) * hn)
+                    ns = slice(h, FC * (CB // 2), 2) if j == NB - 1 else slice(h * hn, (h + 1) * hn)
                     nc.vector.tensor_tensor(out=ucq[:, ns, :], in0=tvq[:, ns, 0, 0:P], in1=tvq[:, ns, 1, 0:P], op=ALU.add)
 
             def turn_out(ob, i, c):
@@ -341,10 +341,11 @@ def tile_graphconvolutionbatch_kernel(tc, H_bytes, H_scale, W, gamma, beta, out)
                 dsel = 1 if (c == 0 or c == COLS - 1) else 0
                 nc.scalar.activation(out=ob[:, i, :], in_=o[:], func=ACT.Copy, scale=dcol[:, dsel : dsel + 1])
 
-            def store(ob, c0, n):
+            def store(ob, i0, c0, n):
                 for b in range(BATCH):
                     nc.sync.dma_start(
-                        out=out[b].rearrange("(r c) f -> r c f", c=COLS)[:, c0 : c0 + n, :], in_=ob[b:P:BATCH, 0:n, :]
+                        out=out[b].rearrange("(r c) f -> r c f", c=COLS)[:, c0 : c0 + n, :],
+                        in_=ob[b:P:BATCH, i0 : i0 + n, :],
                     )
 
             for f in range(FC):
@@ -371,5 +372,8 @@ def tile_graphconvolutionbatch_kernel(tc, H_bytes, H_scale, W, gamma, beta, out)
                     part = cs[:lo] if h == 0 else cs[lo:]
                     for c in part:
                         turn_out(ob, c - cs[0], c)
-                if cs:
-                    store(ob, cs[0], len(cs))
+                        if grp == NB - 1 and c >= COLS - 3:
+                            first = cs[0] if c == COLS - 3 else c
+                            store(ob, first - cs[0], first, c + 1 - first)
+                if cs and grp < NB - 1:
+                    store(ob, 0, cs[0], len(cs))

@@ -24,6 +24,7 @@ HP = HALF + 4
 NPL = FC * CB * HP
 ZW = 2 * NPL + 12
 NZ = 4
+FS = FC - 1
 EPS_BN = 1e-5
 D9 = (9.0 + 1e-5) ** -0.5
 D6 = (6.0 + 1e-5) ** -0.5
@@ -168,15 +169,27 @@ def tile_graphconvolutionbatch_kernel(tc, H_bytes, H_scale, W, gamma, beta, out)
                 nc.vector.quantize_mx(out=codes[:, cols].bitcast(FP8X4), scales=hsc[:, cols], in_=grouped[j][:])
 
             def column_sum(c):
-                nc.tensor.matmul_mx(
-                    out=colsum[:],
-                    lhsT=codes[:, c * P : (c + 1) * P].bitcast(FP8X4),
-                    lhsT_scale=hsc[:, c * P : (c + 1) * P],
-                    rhs=w_codes[:].bitcast(FP8X4),
-                    rhs_scale=w_sc[:],
-                    start=(c == 0),
-                    stop=(c == COLS - 1),
-                )
+                for lo, hi in ((0, 2 * P), (2 * P, FS * P)):
+                    nc.tensor.matmul_mx(
+                        out=colsum[:, lo:hi],
+                        lhsT=codes[:, c * P : (c + 1) * P].bitcast(FP8X4),
+                        lhsT_scale=hsc[:, c * P : (c + 1) * P],
+                        rhs=w_codes[:, lo:hi].bitcast(FP8X4),
+                        rhs_scale=w_sc[:, lo:hi],
+                        start=(c == 0 and lo == 0),
+                        stop=(c == COLS - 1 and lo > 0),
+                    )
+
+            trip = one.tile([P, NB, 6], F32)
+            waiting = {}
+
+            def multiply_last(j):
+                y = py.tile([P, 512], F32, name="y")
+                mx_features(y, FS, j * 512)
+                waiting[j] = y
+
+            def moments(j):
+                nc.vector.bn_stats(out=trip[:, j, :], in_=waiting[j][:])
 
             def square(j, f):
                 y = py.tile([P, 512], F32, name="y")
@@ -194,6 +207,8 @@ def tile_graphconvolutionbatch_kernel(tc, H_bytes, H_scale, W, gamma, beta, out)
                     )
                 if s >= 1:
                     quantise(s - 1)
+                if s >= 2:
+                    moments(s - 2)
                 if s == 5:
                     small_constants()
                 if s >= 1:
@@ -201,7 +216,8 @@ def tile_graphconvolutionbatch_kernel(tc, H_bytes, H_scale, W, gamma, beta, out)
                     if j == NB - 1:
                         for cl in range(CB):
                             column_sum(j * CB + cl)
-                        for f in range(FC):
+                        multiply_last(j)
+                        for f in range(FS):
                             square(j, f)
                     else:
                         square(j, 0)
@@ -210,30 +226,35 @@ def tile_graphconvolutionbatch_kernel(tc, H_bytes, H_scale, W, gamma, beta, out)
                         column_sum(j * CB + 1)
                         square(j, 2)
                         column_sum(j * CB + 2)
-                        square(j, 3)
+                        multiply_last(j)
                         column_sum(j * CB + 3)
 
-            cs_sb = one.tile([P, NF], F32)
-            nc.vector.tensor_copy(out=cs_sb[:], in_=colsum[:])
-            cst = pt.tile([P, FC, P], F32, name="turned")
-            for f in range(FC):
+            cs_sb = one.tile([P, FS * P], F32)
+            nc.vector.tensor_copy(out=cs_sb[:], in_=colsum[:, 0 : FS * P])
+            moments(NB - 1)
+            cst = pt.tile([P, FS, P], F32, name="turned")
+            for f in range(FS):
                 nc.tensor.transpose(cst[:, f, :], cs_sb[:, f * P : (f + 1) * P], ident[:])
-            sum4 = one.tile([P, FC], F32)
-            nc.vector.tensor_reduce(out=sum4[:], in_=cst[:], axis=AX.X, op=ALU.add)
+            mv = one.tile([P, 2], F32)
+            nc.vector.bn_aggr(out=mv[:], in_=trip[:].rearrange("p j k -> p (j k)"))
+            sums = one.tile([P, FS], F32)
+            nc.vector.tensor_reduce(out=sums[:], in_=cst[:], axis=AX.X, op=ALU.add)
             nmean = one.tile([P, FC], F32)
-            nc.vector.tensor_scalar(out=nmean[:], in0=sum4[:], scalar1=-1.0 / NODES, scalar2=None, op0=ALU.mult)
-            m2 = one.tile([P, FC], F32)
-            nc.vector.tensor_tensor(out=m2[:], in0=nmean[:], in1=nmean[:], op=ALU.mult)
+            nc.vector.tensor_scalar(out=nmean[:, FS:FC], in0=mv[:, 0:1], scalar1=-1.0, scalar2=None, op0=ALU.mult)
+            nc.vector.tensor_scalar(out=nmean[:, 0:FS], in0=sums[:], scalar1=-1.0 / NODES, scalar2=None, op0=ALU.mult)
+            ve = one.tile([P, FC], F32)
+            nc.vector.tensor_scalar(out=ve[:, FS:FC], in0=mv[:, 1:2], scalar1=0.0, scalar2=EPS_BN, op0=ALU.max, op1=ALU.add)
+            m2 = one.tile([P, FS], F32)
+            nc.vector.tensor_tensor(out=m2[:], in0=nmean[:, 0:FS], in1=nmean[:, 0:FS], op=ALU.mult)
             gm = one.tile([P, FC], F32)
             nc.vector.tensor_tensor(out=gm[:], in0=nmean[:], in1=g9[:], op=ALU.mult)
-            ssq4 = one.tile([P, FC], F32)
-            nc.vector.tensor_reduce(out=ssq4[:], in_=ssq[:], axis=AX.X, op=ALU.add)
-            var = one.tile([P, FC], F32)
+            ssq4 = one.tile([P, FS], F32)
+            nc.vector.tensor_reduce(out=ssq4[:], in_=ssq[:, 0:FS, :], axis=AX.X, op=ALU.add)
+            var = one.tile([P, FS], F32)
             nc.vector.scalar_tensor_tensor(
                 out=var[:], in0=ssq4[:], scalar=1.0 / NODES, in1=m2[:], op0=ALU.mult, op1=ALU.subtract
             )
-            ve = one.tile([P, FC], F32)
-            nc.vector.tensor_scalar(out=ve[:], in0=var[:], scalar1=0.0, scalar2=EPS_BN, op0=ALU.max, op1=ALU.add)
+            nc.vector.tensor_scalar(out=ve[:, 0:FS], in0=var[:], scalar1=0.0, scalar2=EPS_BN, op0=ALU.max, op1=ALU.add)
             rstd = one.tile([P, FC], F32)
             nc.gpsimd.tensor_tensor(out=rstd[:], in0=ve[:], in1=mhalf[:], op=ALU.pow)
             nc.vector.tensor_tensor(out=a9[:], in0=g9[:], in1=rstd[:], op=ALU.mult)

@@ -264,8 +264,8 @@ def tile_graphconvolutionbatch_kernel(tc, H_bytes, H_scale, W, gamma, beta, out)
 
         with ExitStack() as p2:
             up = p2.enter_context(tc.tile_pool(name="up", bufs=2))
-            tvp = p2.enter_context(tc.tile_pool(name="tvp", bufs=5))
-            ucp = p2.enter_context(tc.tile_pool(name="ucp", bufs=4))
+            tvp = p2.enter_context(tc.tile_pool(name="tvp", bufs=6))
+            ucp = p2.enter_context(tc.tile_pool(name="ucp", bufs=5))
             obp = p2.enter_context(tc.tile_pool(name="obp", bufs=3))
 
             tv_tiles = {}
@@ -304,41 +304,35 @@ def tile_graphconvolutionbatch_kernel(tc, H_bytes, H_scale, W, gamma, beta, out)
                     nc.vector.tensor_scalar(out=ctop, in0=ctop, scalar1=KAPPA, scalar2=None, op0=ALU.mult)
                     nc.vector.tensor_scalar(out=cbot, in0=cbot, scalar1=KAPPA, scalar2=None, op0=ALU.mult)
 
-            def row_sums(j):
+            u_tiles = {}
+
+            def two_rows(j):
                 zb = z_bufs[j % NZ]
                 u = up.tile([P, NPL], F32, name="u")
+                u_tiles[j] = u
+                nc.vector.tensor_tensor(
+                    out=u[:], in0=zb[:, 4 + NPL : 4 + 2 * NPL], in1=zb[:, 4 : 4 + NPL], op=ALU.add
+                )
+
+            def three_rows(j):
+                zb = z_bufs[j % NZ]
                 tv = tvp.tile([P, 2 * NPL], F32, name="tv")
                 tv_tiles[j] = tv
-                hn = NPL // 2
-                for h in range(2):
-                    nc.vector.tensor_tensor(
-                        out=u[:, h * hn : (h + 1) * hn],
-                        in0=zb[:, 4 + NPL + h * hn : 4 + NPL + (h + 1) * hn],
-                        in1=zb[:, 4 + h * hn : 4 + (h + 1) * hn],
-                        op=ALU.add,
-                    )
-                hq = NPL // 4
-                for h in range(2):
-                    nc.vector.tensor_tensor(
-                        out=tv[:, h * NPL : (h + 1) * NPL].rearrange("p (q e b) -> p q e b", e=2, b=BATCH),
-                        in0=u[:, h * hn : (h + 1) * hn]
-                        .rearrange("p (q b) -> p q b", b=BATCH)
-                        .unsqueeze(2)
-                        .to_broadcast([P, hq, 2, BATCH]),
-                        in1=zb[:, 2 : 2 + 2 * (NPL + 4)].rearrange("p (s q b) -> p q s b", s=2, b=BATCH)[
-                            :, h * hq : (h + 1) * hq, :, :
-                        ],
-                        op=ALU.add,
-                    )
+                nq = NPL // 2
+                nc.vector.tensor_tensor(
+                    out=tv[:].rearrange("p (q e b) -> p q e b", e=2, b=BATCH),
+                    in0=u_tiles[j][:].rearrange("p (q b) -> p q b", b=BATCH).unsqueeze(2).to_broadcast([P, nq, 2, BATCH]),
+                    in1=zb[:, 2 : 2 + 2 * (NPL + 4)].rearrange("p (s q b) -> p q s b", s=2, b=BATCH)[:, 0:nq, :, :],
+                    op=ALU.add,
+                )
 
             def column_pairs(j):
                 uc = ucp.tile([P, FC * (CB // 2) * P], F32, name="uc")
                 uc_tiles[j] = uc
                 tvq = tv_tiles[j][:].rearrange("p (n e x) -> p n e x", e=2, x=2 * HP)
                 ucq = uc[:].rearrange("p (n m) -> p n m", m=P)
-                hn = FC * (CB // 2) // 2
-                for h in range(2):
-                    ns = slice(h, FC * (CB // 2), 2) if j == NB - 1 else slice(h * hn, (h + 1) * hn)
+                parts = [slice(0, FC * (CB // 2), 2), slice(1, FC * (CB // 2), 2)] if j == NB - 1 else [slice(0, FC * (CB // 2))]
+                for ns in parts:
                     nc.vector.tensor_tensor(out=ucq[:, ns, :], in0=tvq[:, ns, 0, 0:P], in1=tvq[:, ns, 1, 0:P], op=ALU.add)
 
             def turn_out(ob, i, c):
@@ -371,14 +365,18 @@ def tile_graphconvolutionbatch_kernel(tc, H_bytes, H_scale, W, gamma, beta, out)
 
             for f in range(FC):
                 norm_relu(0, f)
-            for j in range(NB + 2):
+            for j in range(NB + 3):
+                if j == 0:
+                    border_weights(0)
                 if 1 <= j <= NB:
-                    border_weights(j - 1)
+                    two_rows(j - 1)
+                if 1 <= j < NB:
+                    border_weights(j)
                 if 2 <= j <= NB + 1:
                     column_pairs(j - 2)
                 if 1 <= j <= NB:
-                    row_sums(j - 1)
-                grp = j - 2
+                    three_rows(j - 1)
+                grp = j - 3
                 cs = []
                 if grp >= 0:
                     cs = list(range(max(CB * grp - 1, 0), COLS if grp == NB - 1 else CB * grp + CB - 1))

@@ -17,12 +17,14 @@ P = 128
 BATCH, ROWS, COLS, K, NF = 2, 64, 64, 512, 512
 NODES = BATCH * ROWS * COLS
 FC = NF // P
-CB = 4
-NB = COLS // CB
+TB = 2
+NT = COLS // 2
+NB = NT // TB
 HALF = P // 2
-HP = HALF + 4
-NPL = FC * CB * HP
-ZW = 2 * NPL + 12
+RUN = TB * P
+DO = 4
+DE = DO + RUN + HALF - 2
+ZR = 648
 NZ = 4
 FS = FC - 1
 EPS_BN = 1e-5
@@ -39,9 +41,7 @@ def tile_graphconvolutionbatch_kernel(tc, H_bytes, H_scale, W, gamma, beta, out)
     nc = tc.nc
     with ExitStack() as ctx:
         keep = ctx.enter_context(tc.tile_pool(name="keep", bufs=1))
-        py = ctx.enter_context(tc.psum_pool(name="py", bufs=4))
-        pt = ctx.enter_context(tc.psum_pool(name="pt", bufs=3))
-        pm = ctx.enter_context(tc.psum_pool(name="pm", bufs=1))
+        py = ctx.enter_context(tc.psum_pool(name="py", bufs=2))
         ctx.enter_context(tc.manual_schedule())
         ident = keep.tile([P, P], F32)
         perm = keep.tile([P, P], F32)
@@ -52,11 +52,25 @@ def tile_graphconvolutionbatch_kernel(tc, H_bytes, H_scale, W, gamma, beta, out)
         ssq = keep.tile([P, FC, NB], F32)
         a9 = keep.tile([P, FC], F32)
         b9 = keep.tile([P, FC], F32)
+        a6 = keep.tile([P, FC], F32)
+        b6 = keep.tile([P, FC], F32)
         dcol = keep.tile([P, 2], F32)
+        fac = keep.tile([P, 2], F32)
         z_bufs = []
-        for i in range(NZ):
-            zb = keep.tile([P, ZW], F32, name="z_buf%d" % i)
+        for i in range(NZ + 1):
+            zb = keep.tile([P, FC, ZR], F32, name="z_buf%d" % i)
             z_bufs.append(zb)
+
+        def pads(zb):
+            return zb[:, :, DO - 2 : DO - 2 + 10 * HALF].rearrange("p f (k x) -> p f k x", x=HALF)[:, :, :, 0:2]
+
+        def ends(zb, f0, f1):
+            return zb[:, f0:f1, DO + HALF - 2 : DO + HALF - 2 + 8 * HALF].rearrange("p f (k x) -> p f k x", x=HALF)[:, :, :, 0:2]
+
+        def planes(zb, f):
+            return zb[:, f, DO : DO + 2 * (DE - DO)].rearrange("p (s y) -> p s y", s=2)[:, :, 0:RUN].rearrange(
+                "p s (t x) -> p s t x", t=TB
+            )
 
         def mx_features(y, f, n0):
             nc.tensor.matmul_mx(
@@ -70,6 +84,9 @@ def tile_graphconvolutionbatch_kernel(tc, H_bytes, H_scale, W, gamma, beta, out)
             )
 
         with ExitStack() as p1:
+            pt = p1.enter_context(tc.psum_pool(name="pt", bufs=3))
+            py1 = p1.enter_context(tc.psum_pool(name="py1", bufs=2))
+            pm = p1.enter_context(tc.psum_pool(name="pm", bufs=1))
             one = p1.enter_context(tc.tile_pool(name="one", bufs=1))
             hbp = p1.enter_context(tc.tile_pool(name="hbp", bufs=NB))
             hwp = p1.enter_context(tc.tile_pool(name="hwp", bufs=3))
@@ -82,8 +99,9 @@ def tile_graphconvolutionbatch_kernel(tc, H_bytes, H_scale, W, gamma, beta, out)
             h_bytes_sb = []
             w_raw = one.tile([P, 4, NF], BF16)
             for j in range(NB):
-                hb = hbp.tile([P, CB * K], U8, name="h_bytes_tile")
-                nc.sync.dma_start(out=hb[:], in_=hv[:, j * CB * K : (j + 1) * CB * K])
+                hb = hbp.tile([P, 4 * K], U8, name="h_bytes_tile")
+                for h, c0 in enumerate((30 - 2 * j, 32 + 2 * j)):
+                    nc.sync.dma_start(out=hb[:, h * 2 * K : (h + 1) * 2 * K], in_=hv[:, c0 * K : (c0 + 2) * K])
                 h_bytes_sb.append(hb)
                 if j == 0:
                     nc.sync.dma_start(out=w_raw[:], in_=W.rearrange("(p j) n -> p j n", j=4))
@@ -96,22 +114,20 @@ def tile_graphconvolutionbatch_kernel(tc, H_bytes, H_scale, W, gamma, beta, out)
             make_identity(nc, ident[:])
             for s in range(2):
                 nc.vector.tensor_copy(
-                    out=perm[:, s * HALF : (s + 1) * HALF].rearrange("p (i b) -> p b i", b=BATCH),
-                    in_=ident[:].rearrange("p (b i t) -> p b i t", b=BATCH, t=2)[:, :, :, 1 - s],
+                    out=perm[:, s * HALF : (s + 1) * HALF],
+                    in_=ident[:].rearrange("p (bi t) -> p bi t", t=2)[:, :, 1 - s],
                 )
             nc.scalar.copy(out=sb4[:, K : 2 * K], in_=sb4[:, 0:K])
             nc.scalar.copy(out=sb4[:, 2 * K : 4 * K], in_=sb4[:, 0 : 2 * K])
             w_grp = one.tile([P, NF, 4], BF16, align_bytes=64)
             nc.scalar.copy(out=w_grp[:], in_=w_raw[:].rearrange("p j n -> p n j"))
             for zb in z_bufs:
-                nc.gpsimd.memset(zb[:, 0:4], 0.0)
-                nc.gpsimd.memset(zb[:, 4 : 4 + 2 * NPL].rearrange("p (m x) -> p m x", x=HP)[:, :, HALF:HP], 0.0)
-                nc.gpsimd.memset(zb[:, 4 + 2 * NPL : ZW], 0.0)
+                nc.gpsimd.memset(pads(zb), 0.0)
             mhalf = one.tile([P, FC], F32)
             nc.gpsimd.memset(mhalf[:], -0.5)
             g9 = one.tile([P, FC], F32)
             bet9 = one.tile([P, FC], F32)
-            edge = one.tile([P, 1], F32)
+            edge = one.tile([P, 2], F32)
 
             colsum = pm.tile([P, NF], F32, name="colsum")
             widened = {}
@@ -120,24 +136,21 @@ def tile_graphconvolutionbatch_kernel(tc, H_bytes, H_scale, W, gamma, beta, out)
             def small_constants():
                 nc.vector.tensor_scalar(out=g9[:], in0=gam_bf[:], scalar1=D9, scalar2=None, op0=ALU.mult)
                 nc.vector.tensor_scalar(out=bet9[:], in0=bet_bf[:], scalar1=D9, scalar2=None, op0=ALU.mult)
-                nc.vector.tensor_reduce(
-                    out=edge[:],
-                    in_=ident[:].rearrange("p (g w) -> p g w", w=2)[:, 0 : HALF : HALF - 1, :],
-                    axis=AX.XY,
-                    op=ALU.add,
-                )
-                nc.vector.tensor_scalar(
-                    out=dcol[:, 0:1], in0=edge[:], scalar1=D6 - D9, scalar2=D9, op0=ALU.mult, op1=ALU.add
-                )
-                nc.vector.tensor_scalar(
-                    out=dcol[:, 1:2], in0=edge[:], scalar1=D4 - D6, scalar2=D6, op0=ALU.mult, op1=ALU.add
-                )
+                for e in range(2):
+                    nc.vector.tensor_reduce(
+                        out=edge[:, e : e + 1],
+                        in_=ident[:].rearrange("p (b i h) -> p b i h", b=BATCH, h=2)[:, :, 31 * e, :],
+                        axis=AX.XY,
+                        op=ALU.add,
+                    )
+                nc.vector.tensor_scalar(out=dcol[:], in0=edge[:], scalar1=D6 - D9, scalar2=D9, op0=ALU.mult, op1=ALU.add)
+                nc.vector.tensor_scalar(out=fac[:], in0=edge[:], scalar1=D4 / D6 - RHO, scalar2=RHO, op0=ALU.mult, op1=ALU.add)
 
             def widen(j):
-                hw = hwp.tile([P, CB * K], BF16, name="hw")
+                hw = hwp.tile([P, 4 * K], BF16, name="hw")
                 hb = h_bytes_sb[j]
                 if j == 0:
-                    for cl in range(CB):
+                    for cl in range(4):
                         cols = slice(cl * K, (cl + 1) * K)
                         nc.vector.tensor_tensor(
                             out=hw[:, cols], in0=hb[:, cols].bitcast(FP8), in1=sb4[:, 0:K], op=ALU.mult
@@ -148,24 +161,24 @@ def tile_graphconvolutionbatch_kernel(tc, H_bytes, H_scale, W, gamma, beta, out)
 
             def turn_in(j):
                 words = widened[j][:].bitcast(F32)
-                g = gp.tile([P, CB * K], BF16, align_bytes=64, name="g")
+                g = gp.tile([P, 4 * K], BF16, align_bytes=64, name="g")
                 gw = g[:].bitcast(F32)
-                for q in range(CB // 2):
+                for tt in range(TB):
                     xt = pt.tile([P, 2, 2, P], F32, name="turned")
-                    for cc in range(2):
-                        cl = 2 * q + cc
+                    for h in range(2):
+                        cl = 2 * h + (tt if h else 1 - tt)
                         for u in range(2):
                             nc.tensor.transpose(
-                                xt[:, cc, u, :], words[:, cl * (K // 2) + u : (cl + 1) * (K // 2) : 2], perm[:]
+                                xt[:, h, u, :], words[:, cl * (K // 2) + u : (cl + 1) * (K // 2) : 2], perm[:]
                             )
                     nc.scalar.copy(
-                        out=gw[:, q * K : (q + 1) * K].rearrange("p (c r u) -> p c r u", c=2, u=2),
-                        in_=xt[:].rearrange("p c u r -> p c r u"),
+                        out=gw[:, tt * K : (tt + 1) * K].rearrange("p (r x) -> p r x", x=4),
+                        in_=xt[:].rearrange("p h u r -> p r (h u)"),
                     )
                 grouped[j] = g
 
             def quantise(j):
-                cols = slice(j * CB * P, (j + 1) * CB * P)
+                cols = slice(j * 4 * P, (j + 1) * 4 * P)
                 nc.vector.quantize_mx(out=codes[:, cols].bitcast(FP8X4), scales=hsc[:, cols], in_=grouped[j][:])
 
             def column_sum(c):
@@ -183,8 +196,18 @@ def tile_graphconvolutionbatch_kernel(tc, H_bytes, H_scale, W, gamma, beta, out)
             trip = one.tile([P, NB, 6], F32)
             waiting = {}
 
+            count = [0]
+
+            def new_y():
+                count[0] += 1
+                if count[0] % 2:
+                    y = py.tile([P, 512], F32, name="y")
+                else:
+                    y = py1.tile([P, 512], F32, name="y1")
+                return y
+
             def multiply_last(j):
-                y = py.tile([P, 512], F32, name="y")
+                y = new_y()
                 mx_features(y, FS, j * 512)
                 waiting[j] = y
 
@@ -192,7 +215,7 @@ def tile_graphconvolutionbatch_kernel(tc, H_bytes, H_scale, W, gamma, beta, out)
                 nc.vector.bn_stats(out=trip[:, j, :], in_=waiting[j][:])
 
             def square(j, f):
-                y = py.tile([P, 512], F32, name="y")
+                y = new_y()
                 mx_features(y, f, j * 512)
                 junk = jp.tile([P, 512], BF16, name="junk")
                 nc.scalar.activation(out=junk[:], in_=y[:], func=ACT.Square, accum_out=ssq[:, f, j : j + 1])
@@ -214,20 +237,20 @@ def tile_graphconvolutionbatch_kernel(tc, H_bytes, H_scale, W, gamma, beta, out)
                 if s >= 1:
                     j = s - 1
                     if j == NB - 1:
-                        for cl in range(CB):
-                            column_sum(j * CB + cl)
+                        for cl in range(4):
+                            column_sum(j * 4 + cl)
                         multiply_last(j)
                         for f in range(FS):
                             square(j, f)
                     else:
                         square(j, 0)
                         square(j, 1)
-                        column_sum(j * CB)
-                        column_sum(j * CB + 1)
+                        column_sum(j * 4)
+                        column_sum(j * 4 + 1)
                         square(j, 2)
-                        column_sum(j * CB + 2)
+                        column_sum(j * 4 + 2)
                         multiply_last(j)
-                        column_sum(j * CB + 3)
+                        column_sum(j * 4 + 3)
 
             cs_sb = one.tile([P, FS * P], F32)
             nc.vector.tensor_copy(out=cs_sb[:], in_=colsum[:, 0 : FS * P])
@@ -261,138 +284,187 @@ def tile_graphconvolutionbatch_kernel(tc, H_bytes, H_scale, W, gamma, beta, out)
             ma = one.tile([P, FC], F32)
             nc.vector.tensor_tensor(out=ma[:], in0=gm[:], in1=rstd[:], op=ALU.mult)
             nc.vector.tensor_tensor(out=b9[:], in0=bet9[:], in1=ma[:], op=ALU.add)
+            nc.vector.tensor_scalar(out=a6[:], in0=a9[:], scalar1=RHO, scalar2=None, op0=ALU.mult)
+            nc.vector.tensor_scalar(out=b6[:], in0=b9[:], scalar1=RHO, scalar2=None, op0=ALU.mult)
 
         with ExitStack() as p2:
-            up = p2.enter_context(tc.tile_pool(name="up", bufs=2))
-            tvp = p2.enter_context(tc.tile_pool(name="tvp", bufs=6))
-            ucp = p2.enter_context(tc.tile_pool(name="ucp", bufs=5))
-            obp = p2.enter_context(tc.tile_pool(name="obp", bufs=3))
+            pe = p2.enter_context(tc.psum_pool(name="pe", bufs=2))
+            po = p2.enter_context(tc.psum_pool(name="po", bufs=4))
+            up = p2.enter_context(tc.tile_pool(name="up", bufs=5))
+            bp = p2.enter_context(tc.tile_pool(name="bp", bufs=4))
+            pp = p2.enter_context(tc.tile_pool(name="pp", bufs=8))
+            obp = p2.enter_context(tc.tile_pool(name="obp", bufs=4))
 
-            tv_tiles = {}
-            uc_tiles = {}
+            zh = z_bufs[NZ]
+            u_tiles = {}
+            turned = {}
+            pair = {}
+
+            def relu(out_ap, in_ap, f, a, b):
+                nc.scalar.activation(out=out_ap, in_=in_ap, func=ACT.Relu, bias=b[:, f : f + 1], scale=a[:, f : f + 1])
 
             def norm_relu(j, f):
                 zb = z_bufs[j % NZ]
                 y = py.tile([P, 512], F32, name="y")
                 mx_features(y, f, j * 512)
-                nc.scalar.activation(
-                    out=zb[:, 4 : 4 + 2 * NPL].rearrange("p (s n x) -> p n s x", s=2, x=HP)[
-                        :, f * CB : (f + 1) * CB, :, 0:HALF
-                    ],
-                    in_=y[:].rearrange("p (c s x) -> p c s x", c=CB, s=2),
-                    func=ACT.Relu,
-                    bias=b9[:, f : f + 1],
-                    scale=a9[:, f : f + 1],
+                dst = planes(zb, f).rearrange("p s t x -> p t s x")
+                src = y[:].rearrange("p (t s x) -> p t s x", t=TB, s=2)
+                if j == NB - 1:
+                    relu(dst[:, 0, :, :], src[:, 0, :, :], f, a9, b9)
+                    relu(dst[:, 1, :, :], src[:, 1, :, :], f, a6, b6)
+                else:
+                    relu(dst, src, f, a9, b9)
+
+            def swapped_relu(f):
+                y = py.tile([P, 512], F32, name="y")
+                nc.tensor.matmul_mx(
+                    out=y[:, 0 : 2 * P],
+                    lhsT=w_codes[:, f * P : (f + 1) * P].bitcast(FP8X4),
+                    lhsT_scale=w_sc[:, f * P : (f + 1) * P],
+                    rhs=codes[:, 0 : 2 * P].bitcast(FP8X4),
+                    rhs_scale=hsc[:, 0 : 2 * P],
+                    start=True,
+                    stop=True,
+                )
+                relu(
+                    planes(zh, f)[:, :, 0, :].rearrange("p s (x h) -> p s x h", h=2),
+                    y[:, 0 : 2 * P].rearrange("p (s x h) -> p s x h", s=2, h=2)[:, :, :, ::-1],
+                    f,
+                    a9,
+                    b9,
                 )
 
-            def border_weights(j):
-                zb = z_bufs[j % NZ]
-                odd = zb[:, 4 : 4 + NPL]
-                even = zb[:, 4 + NPL : 4 + 2 * NPL]
-                top = even.rearrange("p (n x) -> p n x", x=HP)[:, :, 0:2]
-                bottom = odd.rearrange("p (n x) -> p n x", x=HP)[:, :, HALF - 2 : HALF]
-                nc.vector.tensor_scalar(out=top, in0=top, scalar1=RHO, scalar2=None, op0=ALU.mult)
-                nc.vector.tensor_scalar(out=bottom, in0=bottom, scalar1=RHO, scalar2=None, op0=ALU.mult)
-                if j == 0 or j == NB - 1:
-                    cl = 0 if j == 0 else CB - 1
-                    side = zb[:, 4 : 4 + 2 * NPL].rearrange("p (s f c x) -> p s f c x", s=2, f=FC, c=CB)[
-                        :, :, :, cl, 0:HALF
-                    ]
-                    nc.vector.tensor_scalar(out=side, in0=side, scalar1=RHO, scalar2=None, op0=ALU.mult)
-                    ctop = even.rearrange("p (f c x) -> p f c x", f=FC, c=CB)[:, :, cl, 0:2]
-                    cbot = odd.rearrange("p (f c x) -> p f c x", f=FC, c=CB)[:, :, cl, HALF - 2 : HALF]
-                    nc.vector.tensor_scalar(out=ctop, in0=ctop, scalar1=KAPPA, scalar2=None, op0=ALU.mult)
-                    nc.vector.tensor_scalar(out=cbot, in0=cbot, scalar1=KAPPA, scalar2=None, op0=ALU.mult)
-
-            u_tiles = {}
-
-            def two_rows(j):
-                zb = z_bufs[j % NZ]
-                u = up.tile([P, NPL], F32, name="u")
+            def new_u(j):
+                u = up.tile([P, FC, RUN], F32, name="u")
                 u_tiles[j] = u
-                nc.vector.tensor_tensor(
-                    out=u[:], in0=zb[:, 4 + NPL : 4 + 2 * NPL], in1=zb[:, 4 : 4 + NPL], op=ALU.add
+
+            def two_rows_first():
+                zb = z_bufs[0]
+                new_u(0)
+                for f in range(FC + 1):
+                    if f < FC:
+                        e = ends(zb, f, f + 1)
+                        nc.vector.tensor_scalar(out=e, in0=e, scalar1=RHO, scalar2=None, op0=ALU.mult)
+                    if f > 0:
+                        nc.vector.tensor_tensor(
+                            out=u_tiles[0][:, f - 1, :],
+                            in0=zb[:, f - 1, DE : DE + RUN],
+                            in1=zb[:, f - 1, DO : DO + RUN],
+                            op=ALU.add,
+                        )
+                        nc.vector.memset(ends(zb, f - 1, f), 0.0)
+
+            def two_rows(j, f0, f1):
+                zb = zh if j < 0 else z_bufs[j % NZ]
+                n = P if j < 0 else RUN
+                if j == NB - 1:
+                    for row63 in range(2):
+                        at = DO + P + HALF - 2 if row63 else DE + P
+                        corner = zb[:, f0:f1, at : at + P].rearrange("p f (b x) -> p f b x", b=BATCH)[:, :, :, 0:2]
+                        nc.gpsimd.tensor_scalar(out=corner, in0=corner, scalar1=KAPPA, scalar2=0.0, op0=ALU.mult, op1=ALU.add)
+                e = ends(zb, f0, f1)
+                nc.gpsimd.tensor_scalar(out=e, in0=e, scalar1=RHO, scalar2=0.0, op0=ALU.mult, op1=ALU.add)
+                nc.gpsimd.tensor_tensor(
+                    out=u_tiles[j][:, f0:f1, 0:n], in0=zb[:, f0:f1, DE : DE + n], in1=zb[:, f0:f1, DO : DO + n], op=ALU.add
                 )
+                nc.gpsimd.memset(e, 0.0)
 
-            def three_rows(j):
-                zb = z_bufs[j % NZ]
-                tv = tvp.tile([P, 2 * NPL], F32, name="tv")
-                tv_tiles[j] = tv
-                nq = NPL // 2
-                nc.vector.tensor_tensor(
-                    out=tv[:].rearrange("p (q e b) -> p q e b", e=2, b=BATCH),
-                    in0=u_tiles[j][:].rearrange("p (q b) -> p q b", b=BATCH).unsqueeze(2).to_broadcast([P, nq, 2, BATCH]),
-                    in1=zb[:, 2 : 2 + 2 * (NPL + 4)].rearrange("p (s q b) -> p q s b", s=2, b=BATCH)[:, 0:nq, :, :],
-                    op=ALU.add,
-                )
-
-            def column_pairs(j):
-                uc = ucp.tile([P, FC * (CB // 2) * P], F32, name="uc")
-                uc_tiles[j] = uc
-                tvq = tv_tiles[j][:].rearrange("p (n e x) -> p n e x", e=2, x=2 * HP)
-                ucq = uc[:].rearrange("p (n m) -> p n m", m=P)
-                parts = [slice(0, FC * (CB // 2), 2), slice(1, FC * (CB // 2), 2)] if j == NB - 1 else [slice(0, FC * (CB // 2))]
-                for ns in parts:
-                    nc.vector.tensor_tensor(out=ucq[:, ns, :], in0=tvq[:, ns, 0, 0:P], in1=tvq[:, ns, 1, 0:P], op=ALU.add)
-
-            def turn_out(ob, i, c):
-                o = pt.tile([P, NF], F32, name="turned")
-                cn = c - 1 if c % 2 == 0 else c + 1
+            def turn_out(t, e):
+                j = -1 if t < 0 else t // TB
+                tt = 0 if t < 0 else t % TB
+                zb = zh if t < 0 else z_bufs[j % NZ]
+                if t < 0:
+                    o = py.tile([P, NF], F32, name="y")
+                elif t % 2 == 0:
+                    o = pe.tile([P, NF], F32, name="turned_even")
+                else:
+                    o = po.tile([P, NF], F32, name="turned_odd")
                 for f in range(FC):
-                    n_uc = f * (CB // 2) + (c % CB) // 2
-                    wins = [uc_tiles[c // CB][:, n_uc * P : (n_uc + 1) * P]]
-                    if 0 <= cn < COLS:
-                        n_tv = f * CB + cn % CB
-                        wins.append(tv_tiles[cn // CB][:, n_tv * 2 * HP : n_tv * 2 * HP + P])
-                    for w in range(len(wins)):
+                    w0 = (DE + 2 if e else DO - 2) + tt * P
+                    for w, win in enumerate((u_tiles[j][:, f, tt * P : (tt + 1) * P], zb[:, f, w0 : w0 + P])):
                         nc.tensor.matmul(
                             out=o[:, f * P : (f + 1) * P],
-                            lhsT=wins[w],
+                            lhsT=win,
                             rhs=ident[:],
                             is_transpose=True,
                             start=(w == 0),
-                            stop=(w == len(wins) - 1),
+                            stop=(w == 1),
                         )
-                dsel = 1 if (c == 0 or c == COLS - 1) else 0
-                nc.scalar.activation(out=ob[:, i, :], in_=o[:], func=ACT.Copy, scale=dcol[:, dsel : dsel + 1])
+                turned[t, e] = o
 
-            def store(ob, i0, c0, n):
-                for b in range(BATCH):
-                    nc.sync.dma_start(
-                        out=out[b].rearrange("(r c) f -> r c f", c=COLS)[:, c0 : c0 + n, :],
-                        in_=ob[b:P:BATCH, i0 : i0 + n, :],
-                    )
+            def add_turned(dst, t, e, other):
+                nc.vector.scalar_tensor_tensor(
+                    out=dst, in0=turned[t, e][:], scalar=dcol[:, e : e + 1], in1=other, op0=ALU.mult, op1=ALU.add
+                )
+
+            out_v = out.rearrange("b (i e c) f -> c (b i) e f", e=2, c=COLS)
+            out_c = out.rearrange("b (i e c) f -> (b i) e (c f)", e=2, c=COLS)
+
+            def store(ob, k0, t, n):
+                for k in range(n):
+                    nc.sync.dma_start(out=out_v[31 - t - k], in_=ob[0:P:2, :, k0 + k, :])
+                nc.sync.dma_start(
+                    out=out_c[:, :, (32 + t) * NF : (32 + t + n) * NF],
+                    in_=ob[1:P:2, :, k0 : k0 + n, :].rearrange("p e k f -> p e (k f)"),
+                )
 
             for f in range(FC):
                 norm_relu(0, f)
-            for j in range(NB + 3):
-                if j == 0:
-                    border_weights(0)
-                if 1 <= j <= NB:
-                    two_rows(j - 1)
-                if 1 <= j < NB:
-                    border_weights(j)
-                if 2 <= j <= NB + 1:
-                    column_pairs(j - 2)
-                if 1 <= j <= NB:
-                    three_rows(j - 1)
-                grp = j - 3
-                cs = []
-                if grp >= 0:
-                    cs = list(range(max(CB * grp - 1, 0), COLS if grp == NB - 1 else CB * grp + CB - 1))
-                ob = None
-                if cs:
-                    ob = obp.tile([P, CB + 1, NF], F32, name="ob")
-                for h in range(2):
-                    if j + 1 < NB:
-                        norm_relu(j + 1, 2 * h)
-                        norm_relu(j + 1, 2 * h + 1)
-                    lo = (len(cs) + 1) // 2
-                    part = cs[:lo] if h == 0 else cs[lo:]
-                    for c in part:
-                        turn_out(ob, c - cs[0], c)
-                        if grp == NB - 1 and c >= COLS - 3:
-                            first = cs[0] if c == COLS - 3 else c
-                            store(ob, first - cs[0], first, c + 1 - first)
-                if cs and grp < NB - 1:
-                    store(ob, 0, cs[0], len(cs))
+            two_rows_first()
+            new_u(1)
+            norm_relu(1, 0)
+            norm_relu(1, 1)
+            for q in range(NB):
+                ob = obp.tile([P, 2, TB, NF], F32, name="ob")
+                if q + 1 < NB:
+                    two_rows(q + 1, 0, 2)
+                    norm_relu(q + 1, 2)
+                    norm_relu(q + 1, 3)
+                    two_rows(q + 1, 2, 4)
+                for e in range(2):
+                    turn_out(TB * q, e)
+                both = {}
+                for e in range(2):
+                    bt = bp.tile([P, NF], F32, name="bt")
+                    nc.scalar.activation(out=bt[:], in_=turned[TB * q, e][:], func=ACT.Copy, scale=dcol[:, e : e + 1])
+                    both[e] = bt
+                if q > 0:
+                    for e in range(2):
+                        add_turned(ob[:, e, 0, :], TB * q, e, pair[q - 1, e][:])
+                if q == NB - 1:
+                    store(ob, 0, TB * q - 1, 1)
+                if q == 1:
+                    for f in range(FC):
+                        swapped_relu(f)
+                    new_u(-1)
+                    two_rows(-1, 0, FC)
+                if q + 2 < NB:
+                    new_u(q + 2)
+                    norm_relu(q + 2, 0)
+                    norm_relu(q + 2, 1)
+                for e in range(2):
+                    turn_out(TB * q + 1, e)
+                if q == 2:
+                    for e in range(2):
+                        turn_out(-1, e)
+                for e in range(2):
+                    pr = pp.tile([P, NF], F32, name="pr")
+                    add_turned(pr[:], TB * q + 1, e, both[e][:])
+                    pair[q, e] = pr
+                if q == NB - 1:
+                    last = obp.tile([P, 2, TB, NF], F32, name="ob")
+                    for e in range(2):
+                        nc.scalar.activation(out=last[:, e, 0, :], in_=pair[q, e][:], func=ACT.Copy, scale=fac[:, e : e + 1])
+                if q > 0:
+                    for e in range(2):
+                        add_turned(ob[:, e, 1, :], TB * q - 1, e, pair[q, e][:])
+                if q == 2:
+                    first = obp.tile([P, 2, TB, NF], F32, name="ob")
+                    for e in range(2):
+                        add_turned(first[:, e, 0, :], -1, e, pair[0, e][:])
+                    store(first, 0, 0, 1)
+                if q == NB - 1:
+                    store(ob, 1, TB * q, 1)
+                    store(last, 0, NT - 1, 1)
+                elif q > 0:
+                    store(ob, 0, TB * q - 1, TB)

@@ -20,11 +20,12 @@ FC = NF // P
 TB = 2
 NT = COLS // 2
 NB = NT // TB
-HALF = P // 2
+IB = P // 2
+MAIN = P - 4
 RUN = TB * P
-DO = 4
-DE = DO + RUN + HALF - 2
-ZR = 648
+RS = P + 4
+EV = TB * RS
+ZR = 2 * EV + 8
 NZ = 4
 FS = FC - 1
 EPS_BN = 1e-5
@@ -32,7 +33,6 @@ D9 = (9.0 + 1e-5) ** -0.5
 D6 = (6.0 + 1e-5) ** -0.5
 D4 = (4.0 + 1e-5) ** -0.5
 RHO = D6 / D9
-KAPPA = (D4 / D9) / (RHO * RHO)
 
 FLOPS = 2 * NODES * K * NF
 
@@ -54,6 +54,8 @@ def tile_graphconvolutionbatch_kernel(tc, H_bytes, H_scale, W, gamma, beta, out)
         b9 = keep.tile([P, FC], F32)
         a6 = keep.tile([P, FC], F32)
         b6 = keep.tile([P, FC], F32)
+        a4 = keep.tile([P, FC], F32)
+        b4 = keep.tile([P, FC], F32)
         dcol = keep.tile([P, 2], F32)
         fac = keep.tile([P, 2], F32)
         z_bufs = []
@@ -61,16 +63,11 @@ def tile_graphconvolutionbatch_kernel(tc, H_bytes, H_scale, W, gamma, beta, out)
             zb = keep.tile([P, FC, ZR], F32, name="z_buf%d" % i)
             z_bufs.append(zb)
 
-        def pads(zb):
-            return zb[:, :, DO - 2 : DO - 2 + 10 * HALF].rearrange("p f (k x) -> p f k x", x=HALF)[:, :, :, 0:2]
+        def odd(zb):
+            return zb[:, :, 0:EV].rearrange("p f (t x) -> p f t x", x=RS)
 
-        def ends(zb, f0, f1):
-            return zb[:, f0:f1, DO + HALF - 2 : DO + HALF - 2 + 8 * HALF].rearrange("p f (k x) -> p f k x", x=HALF)[:, :, :, 0:2]
-
-        def planes(zb, f):
-            return zb[:, f, DO : DO + 2 * (DE - DO)].rearrange("p (s y) -> p s y", s=2)[:, :, 0:RUN].rearrange(
-                "p s (t x) -> p s t x", t=TB
-            )
+        def even(zb):
+            return zb[:, :, EV : 2 * EV].rearrange("p f (t x) -> p f t x", x=RS)
 
         def mx_features(y, f, n0):
             nc.tensor.matmul_mx(
@@ -112,19 +109,21 @@ def tile_graphconvolutionbatch_kernel(tc, H_bytes, H_scale, W, gamma, beta, out)
                 nc.sync.dma_start(out=bet_bf[:], in_=beta.rearrange("(c p) -> p c", p=P))
 
             make_identity(nc, ident[:])
-            for s in range(2):
+            sorted_ident = ident[:].rearrange("p (b i t) -> p t i b", b=BATCH, t=2)
+            at = 0
+            for parity, i0, i1 in ((1, 0, 31), (0, 1, 32), (1, 31, 32), (0, 0, 1)):
+                n = (i1 - i0) * BATCH
                 nc.vector.tensor_copy(
-                    out=perm[:, s * HALF : (s + 1) * HALF],
-                    in_=ident[:].rearrange("p (bi t) -> p bi t", t=2)[:, :, 1 - s],
+                    out=perm[:, at : at + n].rearrange("p (i b) -> p i b", b=BATCH), in_=sorted_ident[:, parity, i0:i1, :]
                 )
+                at += n
             nc.scalar.copy(out=sb4[:, K : 2 * K], in_=sb4[:, 0:K])
             nc.scalar.copy(out=sb4[:, 2 * K : 4 * K], in_=sb4[:, 0 : 2 * K])
             w_grp = one.tile([P, NF, 4], BF16, align_bytes=64)
             nc.scalar.copy(out=w_grp[:], in_=w_raw[:].rearrange("p j n -> p n j"))
             for zb in z_bufs:
-                nc.gpsimd.memset(pads(zb), 0.0)
-            mhalf = one.tile([P, FC], F32)
-            nc.gpsimd.memset(mhalf[:], -0.5)
+                nc.gpsimd.memset(odd(zb)[:, :, :, 0:4], 0.0)
+                nc.gpsimd.memset(even(zb)[:, :, :, P:RS], 0.0)
             g9 = one.tile([P, FC], F32)
             bet9 = one.tile([P, FC], F32)
             edge = one.tile([P, 2], F32)
@@ -139,8 +138,8 @@ def tile_graphconvolutionbatch_kernel(tc, H_bytes, H_scale, W, gamma, beta, out)
                 for e in range(2):
                     nc.vector.tensor_reduce(
                         out=edge[:, e : e + 1],
-                        in_=ident[:].rearrange("p (b i h) -> p b i h", b=BATCH, h=2)[:, :, 31 * e, :],
-                        axis=AX.XY,
+                        in_=ident[:].rearrange("p (i x) -> p i x", x=4)[:, 31 * e, :],
+                        axis=AX.X,
                         op=ALU.add,
                     )
                 nc.vector.tensor_scalar(out=dcol[:], in0=edge[:], scalar1=D6 - D9, scalar2=D9, op0=ALU.mult, op1=ALU.add)
@@ -279,17 +278,20 @@ def tile_graphconvolutionbatch_kernel(tc, H_bytes, H_scale, W, gamma, beta, out)
             )
             nc.vector.tensor_scalar(out=ve[:, 0:FS], in0=var[:], scalar1=0.0, scalar2=EPS_BN, op0=ALU.max, op1=ALU.add)
             rstd = one.tile([P, FC], F32)
-            nc.gpsimd.tensor_tensor(out=rstd[:], in0=ve[:], in1=mhalf[:], op=ALU.pow)
+            nc.scalar.activation(out=rstd[:], in_=ve[:], func=ACT.Abs_reciprocal_sqrt)
             nc.vector.tensor_tensor(out=a9[:], in0=g9[:], in1=rstd[:], op=ALU.mult)
             ma = one.tile([P, FC], F32)
             nc.vector.tensor_tensor(out=ma[:], in0=gm[:], in1=rstd[:], op=ALU.mult)
             nc.vector.tensor_tensor(out=b9[:], in0=bet9[:], in1=ma[:], op=ALU.add)
             nc.vector.tensor_scalar(out=a6[:], in0=a9[:], scalar1=RHO, scalar2=None, op0=ALU.mult)
             nc.vector.tensor_scalar(out=b6[:], in0=b9[:], scalar1=RHO, scalar2=None, op0=ALU.mult)
+            nc.vector.tensor_scalar(out=a4[:], in0=a9[:], scalar1=D4 / D9, scalar2=None, op0=ALU.mult)
+            nc.vector.tensor_scalar(out=b4[:], in0=b9[:], scalar1=D4 / D9, scalar2=None, op0=ALU.mult)
 
         with ExitStack() as p2:
             pe = p2.enter_context(tc.psum_pool(name="pe", bufs=2))
             po = p2.enter_context(tc.psum_pool(name="po", bufs=4))
+            tvp = p2.enter_context(tc.tile_pool(name="tvp", bufs=4))
             up = p2.enter_context(tc.tile_pool(name="up", bufs=5))
             bp = p2.enter_context(tc.tile_pool(name="bp", bufs=4))
             pp = p2.enter_context(tc.tile_pool(name="pp", bufs=8))
@@ -297,77 +299,71 @@ def tile_graphconvolutionbatch_kernel(tc, H_bytes, H_scale, W, gamma, beta, out)
 
             zh = z_bufs[NZ]
             u_tiles = {}
+            three = {}
             turned = {}
             pair = {}
 
             def relu(out_ap, in_ap, f, a, b):
                 nc.scalar.activation(out=out_ap, in_=in_ap, func=ACT.Relu, bias=b[:, f : f + 1], scale=a[:, f : f + 1])
 
+            def mains(zb, f):
+                return zb[:, f, 0 : 2 * EV].rearrange("p (s t x) -> p t s x", s=2, x=RS)[:, :, :, 4:P]
+
+            def borders(zb, f):
+                return zb[:, f, P : P + 2 * (RS + 4)].rearrange("p (s g x) -> p g s x", s=2, x=4)[:, 0 : RS // 4 + 1 : RS // 4, :, :]
+
             def norm_relu(j, f):
                 zb = z_bufs[j % NZ]
-                y = py.tile([P, 512], F32, name="y")
-                mx_features(y, f, j * 512)
-                dst = planes(zb, f).rearrange("p s t x -> p t s x")
-                src = y[:].rearrange("p (t s x) -> p t s x", t=TB, s=2)
-                if j == NB - 1:
-                    relu(dst[:, 0, :, :], src[:, 0, :, :], f, a9, b9)
-                    relu(dst[:, 1, :, :], src[:, 1, :, :], f, a6, b6)
+                if j == 0:
+                    y = po.tile([P, NF], F32, name="turned_odd")
                 else:
-                    relu(dst, src, f, a9, b9)
-
-            def swapped_relu(f):
-                y = py.tile([P, 512], F32, name="y")
-                nc.tensor.matmul_mx(
-                    out=y[:, 0 : 2 * P],
-                    lhsT=w_codes[:, f * P : (f + 1) * P].bitcast(FP8X4),
-                    lhsT_scale=w_sc[:, f * P : (f + 1) * P],
-                    rhs=codes[:, 0 : 2 * P].bitcast(FP8X4),
-                    rhs_scale=hsc[:, 0 : 2 * P],
-                    start=True,
-                    stop=True,
-                )
-                relu(
-                    planes(zh, f)[:, :, 0, :].rearrange("p s (x h) -> p s x h", h=2),
-                    y[:, 0 : 2 * P].rearrange("p (s x h) -> p s x h", s=2, h=2)[:, :, :, ::-1],
-                    f,
-                    a9,
-                    b9,
-                )
-
-            def new_u(j):
-                u = up.tile([P, FC, RUN], F32, name="u")
-                u_tiles[j] = u
-
-            def two_rows_first():
-                zb = z_bufs[0]
-                new_u(0)
-                for f in range(FC + 1):
-                    if f < FC:
-                        e = ends(zb, f, f + 1)
-                        nc.vector.tensor_scalar(out=e, in0=e, scalar1=RHO, scalar2=None, op0=ALU.mult)
-                    if f > 0:
-                        nc.vector.tensor_tensor(
-                            out=u_tiles[0][:, f - 1, :],
-                            in0=zb[:, f - 1, DE : DE + RUN],
-                            in1=zb[:, f - 1, DO : DO + RUN],
-                            op=ALU.add,
-                        )
-                        nc.vector.memset(ends(zb, f - 1, f), 0.0)
-
-            def two_rows(j, f0, f1):
-                zb = zh if j < 0 else z_bufs[j % NZ]
-                n = P if j < 0 else RUN
+                    y = py.tile([P, 512], F32, name="y")
+                mx_features(y, f, j * 512)
+                src = y[:].rearrange("p (t x) -> p t x", t=TB)
+                src_main = src[:, :, 0 : 2 * MAIN].rearrange("p t (s x) -> p t s x", s=2)
+                src_border = src[:, :, 2 * MAIN : 2 * P].rearrange("p t (s x) -> p t s x", s=2)
                 if j == NB - 1:
-                    for row63 in range(2):
-                        at = DO + P + HALF - 2 if row63 else DE + P
-                        corner = zb[:, f0:f1, at : at + P].rearrange("p f (b x) -> p f b x", b=BATCH)[:, :, :, 0:2]
-                        nc.gpsimd.tensor_scalar(out=corner, in0=corner, scalar1=KAPPA, scalar2=0.0, op0=ALU.mult, op1=ALU.add)
-                e = ends(zb, f0, f1)
-                nc.gpsimd.tensor_scalar(out=e, in0=e, scalar1=RHO, scalar2=0.0, op0=ALU.mult, op1=ALU.add)
-                nc.gpsimd.tensor_tensor(
-                    out=u_tiles[j][:, f0:f1, 0:n], in0=zb[:, f0:f1, DE : DE + n], in1=zb[:, f0:f1, DO : DO + n], op=ALU.add
+                    for t, main, border in ((0, (a9, b9), (a6, b6)), (1, (a6, b6), (a4, b4))):
+                        relu(mains(zb, f)[:, t, :, :], src_main[:, t, :, :], f, *main)
+                        relu(borders(zb, f)[:, t, :, :], src_border[:, t, :, :], f, *border)
+                else:
+                    relu(mains(zb, f), src_main, f, a9, b9)
+                    relu(borders(zb, f), src_border, f, a6, b6)
+
+            def swap_columns(f):
+                def both(zb):
+                    return zb[:, f, 4 : 4 + 2 * (EV - 4)].rearrange("p (s y) -> p s y", s=2)[:, :, 0:P].rearrange(
+                        "p s (x h) -> p s x h", h=2
+                    )
+
+                nc.vector.tensor_copy(out=both(zh), in_=both(z_bufs[0])[:, :, :, ::-1])
+
+            def two_rows(engine, j, f0, f1):
+                if j not in u_tiles:
+                    u = up.tile([P, FC, TB, P], F32, name="u")
+                    u_tiles[j] = u
+                zb = zh if j < 0 else z_bufs[j % NZ]
+                n = 1 if j < 0 else TB
+                engine.tensor_tensor(
+                    out=u_tiles[j][:, f0:f1, 0:n, :],
+                    in0=even(zb)[:, f0:f1, 0:n, 0:P],
+                    in1=odd(zb)[:, f0:f1, 0:n, 4:RS],
+                    op=ALU.add,
                 )
-                nc.gpsimd.memset(e, 0.0)
+
+            def three_rows(engine, j):
+                zb = zh if j < 0 else z_bufs[j % NZ]
+                n = 1 if j < 0 else TB
+                tv = tvp.tile([P, 2, TB, P], F32, name="tv")
+                three[j] = tv
+                engine.tensor_tensor(
+                    out=tv[:, :, 0:n, :],
+                    in0=u_tiles[j][:, 0, 0:n, :].unsqueeze(1).to_broadcast([P, 2, n, P]),
+                    in1=zb[:, 0, 0 : 2 * (EV + 4)].rearrange("p (s y) -> p s y", s=2)[:, :, 0:EV].rearrange(
+                        "p s (t x) -> p s t x", x=RS
+                    )[:, :, 0:n, 0:P],
+                    op=ALU.add,
+                )
 
             def turn_out(t, e):
                 j = -1 if t < 0 else t // TB
@@ -380,15 +376,19 @@ def tile_graphconvolutionbatch_kernel(tc, H_bytes, H_scale, W, gamma, beta, out)
                 else:
                     o = po.tile([P, NF], F32, name="turned_odd")
                 for f in range(FC):
-                    w0 = (DE + 2 if e else DO - 2) + tt * P
-                    for w, win in enumerate((u_tiles[j][:, f, tt * P : (tt + 1) * P], zb[:, f, w0 : w0 + P])):
+                    w0 = EV + 4 if e else 0
+                    if f == 0:
+                        wins = [three[j][:, e, tt, :]]
+                    else:
+                        wins = [u_tiles[j][:, f, tt, :], zb[:, f, w0 + tt * RS : w0 + tt * RS + P]]
+                    for w, win in enumerate(wins):
                         nc.tensor.matmul(
                             out=o[:, f * P : (f + 1) * P],
                             lhsT=win,
                             rhs=ident[:],
                             is_transpose=True,
                             start=(w == 0),
-                            stop=(w == 1),
+                            stop=(w == len(wins) - 1),
                         )
                 turned[t, e] = o
 
@@ -397,30 +397,38 @@ def tile_graphconvolutionbatch_kernel(tc, H_bytes, H_scale, W, gamma, beta, out)
                     out=dst, in0=turned[t, e][:], scalar=dcol[:, e : e + 1], in1=other, op0=ALU.mult, op1=ALU.add
                 )
 
-            out_v = out.rearrange("b (i e c) f -> c (b i) e f", e=2, c=COLS)
-            out_c = out.rearrange("b (i e c) f -> (b i) e (c f)", e=2, c=COLS)
+            out_v = out.rearrange("b (i e c) f -> b c i e f", e=2, c=COLS)
+            out_c = out.rearrange("b (i e c) f -> b i e (c f)", e=2, c=COLS)
 
             def store(ob, k0, t, n):
-                for k in range(n):
-                    nc.sync.dma_start(out=out_v[31 - t - k], in_=ob[0:P:2, :, k0 + k, :])
-                nc.sync.dma_start(
-                    out=out_c[:, :, (32 + t) * NF : (32 + t + n) * NF],
-                    in_=ob[1:P:2, :, k0 : k0 + n, :].rearrange("p e k f -> p e (k f)"),
-                )
+                for b in range(BATCH):
+                    for k in range(n):
+                        nc.sync.dma_start(out=out_v[b, 31 - t - k], in_=ob[2 * b : P : 4, :, k0 + k, :])
+                    nc.sync.dma_start(
+                        out=out_c[b, :, :, (32 + t) * NF : (32 + t + n) * NF],
+                        in_=ob[2 * b + 1 : P : 4, :, k0 : k0 + n, :].rearrange("p e k f -> p e (k f)"),
+                    )
 
             for f in range(FC):
                 norm_relu(0, f)
-            two_rows_first()
-            new_u(1)
+                two_rows(nc.vector, 0, f, f + 1)
+                swap_columns(f)
+            two_rows(nc.vector, -1, 0, FC)
+            three_rows(nc.vector, 0)
+            three_rows(nc.vector, -1)
             norm_relu(1, 0)
             norm_relu(1, 1)
             for q in range(NB):
                 ob = obp.tile([P, 2, TB, NF], F32, name="ob")
+                if q == 0:
+                    norm_relu(1, 2)
+                    norm_relu(1, 3)
+                elif q + 2 < NB:
+                    norm_relu(q + 2, 0)
+                    norm_relu(q + 2, 1)
                 if q + 1 < NB:
-                    two_rows(q + 1, 0, 2)
-                    norm_relu(q + 1, 2)
-                    norm_relu(q + 1, 3)
-                    two_rows(q + 1, 2, 4)
+                    two_rows(nc.gpsimd, q + 1, 0, FC)
+                    three_rows(nc.gpsimd, q + 1)
                 for e in range(2):
                     turn_out(TB * q, e)
                 both = {}
@@ -433,18 +441,18 @@ def tile_graphconvolutionbatch_kernel(tc, H_bytes, H_scale, W, gamma, beta, out)
                         add_turned(ob[:, e, 0, :], TB * q, e, pair[q - 1, e][:])
                 if q == NB - 1:
                     store(ob, 0, TB * q - 1, 1)
-                if q == 1:
-                    for f in range(FC):
-                        swapped_relu(f)
-                    new_u(-1)
-                    two_rows(-1, 0, FC)
-                if q + 2 < NB:
-                    new_u(q + 2)
-                    norm_relu(q + 2, 0)
-                    norm_relu(q + 2, 1)
+                if q == 0:
+                    norm_relu(2, 0)
+                    norm_relu(2, 1)
+                elif q + 2 < NB:
+                    norm_relu(q + 2, 2)
+                    norm_relu(q + 2, 3)
                 for e in range(2):
                     turn_out(TB * q + 1, e)
-                if q == 2:
+                if q == 0:
+                    norm_relu(2, 2)
+                    norm_relu(2, 3)
+                if q == 1:
                     for e in range(2):
                         turn_out(-1, e)
                 for e in range(2):
@@ -458,7 +466,7 @@ def tile_graphconvolutionbatch_kernel(tc, H_bytes, H_scale, W, gamma, beta, out)
                 if q > 0:
                     for e in range(2):
                         add_turned(ob[:, e, 1, :], TB * q - 1, e, pair[q, e][:])
-                if q == 2:
+                if q == 1:
                     first = obp.tile([P, 2, TB, NF], F32, name="ob")
                     for e in range(2):
                         add_turned(first[:, e, 0, :], -1, e, pair[0, e][:])

@@ -21,11 +21,10 @@ TB = 2
 NT = COLS // 2
 NB = NT // TB
 IB = P // 2
-MAIN = P - 4
 RUN = TB * P
 RS = P + 4
-EV = TB * RS
-ZR = 2 * EV + 8
+EV = P + TB * RS - 4
+ZR = 2 * EV
 NZ = 4
 FS = FC - 1
 EPS_BN = 1e-5
@@ -33,6 +32,7 @@ D9 = (9.0 + 1e-5) ** -0.5
 D6 = (6.0 + 1e-5) ** -0.5
 D4 = (4.0 + 1e-5) ** -0.5
 RHO = D6 / D9
+KAPPA = (D4 / D9) / (RHO * RHO)
 
 FLOPS = 2 * NODES * K * NF
 
@@ -54,8 +54,6 @@ def tile_graphconvolutionbatch_kernel(tc, H_bytes, H_scale, W, gamma, beta, out)
         b9 = keep.tile([P, FC], F32)
         a6 = keep.tile([P, FC], F32)
         b6 = keep.tile([P, FC], F32)
-        a4 = keep.tile([P, FC], F32)
-        b4 = keep.tile([P, FC], F32)
         dcol = keep.tile([P, 2], F32)
         fac = keep.tile([P, 2], F32)
         z_bufs = []
@@ -63,11 +61,10 @@ def tile_graphconvolutionbatch_kernel(tc, H_bytes, H_scale, W, gamma, beta, out)
             zb = keep.tile([P, FC, ZR], F32, name="z_buf%d" % i)
             z_bufs.append(zb)
 
-        def odd(zb):
-            return zb[:, :, 0:EV].rearrange("p f (t x) -> p f t x", x=RS)
-
-        def even(zb):
-            return zb[:, :, EV : 2 * EV].rearrange("p f (t x) -> p f t x", x=RS)
+        def runs(zb):
+            return zb[:, :, 0 : 2 * EV].rearrange("p f (s y) -> p f s y", s=2)[:, :, :, 0 : TB * RS].rearrange(
+                "p f s (t x) -> p f s t x", x=RS
+            )
 
         def mx_features(y, f, n0):
             nc.tensor.matmul_mx(
@@ -95,6 +92,7 @@ def tile_graphconvolutionbatch_kernel(tc, H_bytes, H_scale, W, gamma, beta, out)
             hv = H_bytes.rearrange("b (r c) k -> (b r) (c k)", c=COLS)
             h_bytes_sb = []
             w_raw = one.tile([P, 4, NF], BF16)
+            warm = one.tile([P, 2], F32)
             for j in range(NB):
                 hb = hbp.tile([P, 4 * K], U8, name="h_bytes_tile")
                 for h, c0 in enumerate((30 - 2 * j, 32 + 2 * j)):
@@ -108,22 +106,21 @@ def tile_graphconvolutionbatch_kernel(tc, H_bytes, H_scale, W, gamma, beta, out)
                 nc.sync.dma_start(out=gam_bf[:], in_=gamma.rearrange("(c p) -> p c", p=P))
                 nc.sync.dma_start(out=bet_bf[:], in_=beta.rearrange("(c p) -> p c", p=P))
 
+            for zb in z_bufs:
+                nc.vector.memset(runs(zb)[:, :, :, :, 0:4], 0.0)
+                nc.vector.memset(zb[:, :, EV + TB * RS : ZR], 0.0)
+            nc.gpsimd.memset(warm[:, 0:1], 1.0)
+            nc.scalar.activation(out=warm[:, 1:2], in_=warm[:, 0:1], func=ACT.Abs_reciprocal_sqrt)
             make_identity(nc, ident[:])
-            sorted_ident = ident[:].rearrange("p (b i t) -> p t i b", b=BATCH, t=2)
-            at = 0
-            for parity, i0, i1 in ((1, 0, 31), (0, 1, 32), (1, 31, 32), (0, 0, 1)):
-                n = (i1 - i0) * BATCH
+            for s in range(2):
                 nc.vector.tensor_copy(
-                    out=perm[:, at : at + n].rearrange("p (i b) -> p i b", b=BATCH), in_=sorted_ident[:, parity, i0:i1, :]
+                    out=perm[:, s * IB : (s + 1) * IB].rearrange("p (i b) -> p i b", b=BATCH),
+                    in_=ident[:].rearrange("p (b i t) -> p t i b", b=BATCH, t=2)[:, 1 - s, :, :],
                 )
-                at += n
             nc.scalar.copy(out=sb4[:, K : 2 * K], in_=sb4[:, 0:K])
             nc.scalar.copy(out=sb4[:, 2 * K : 4 * K], in_=sb4[:, 0 : 2 * K])
             w_grp = one.tile([P, NF, 4], BF16, align_bytes=64)
             nc.scalar.copy(out=w_grp[:], in_=w_raw[:].rearrange("p j n -> p n j"))
-            for zb in z_bufs:
-                nc.gpsimd.memset(odd(zb)[:, :, :, 0:4], 0.0)
-                nc.gpsimd.memset(even(zb)[:, :, :, P:RS], 0.0)
             g9 = one.tile([P, FC], F32)
             bet9 = one.tile([P, FC], F32)
             edge = one.tile([P, 2], F32)
@@ -285,32 +282,22 @@ def tile_graphconvolutionbatch_kernel(tc, H_bytes, H_scale, W, gamma, beta, out)
             nc.vector.tensor_tensor(out=b9[:], in0=bet9[:], in1=ma[:], op=ALU.add)
             nc.vector.tensor_scalar(out=a6[:], in0=a9[:], scalar1=RHO, scalar2=None, op0=ALU.mult)
             nc.vector.tensor_scalar(out=b6[:], in0=b9[:], scalar1=RHO, scalar2=None, op0=ALU.mult)
-            nc.vector.tensor_scalar(out=a4[:], in0=a9[:], scalar1=D4 / D9, scalar2=None, op0=ALU.mult)
-            nc.vector.tensor_scalar(out=b4[:], in0=b9[:], scalar1=D4 / D9, scalar2=None, op0=ALU.mult)
 
         with ExitStack() as p2:
             pe = p2.enter_context(tc.psum_pool(name="pe", bufs=2))
             po = p2.enter_context(tc.psum_pool(name="po", bufs=4))
-            tvp = p2.enter_context(tc.tile_pool(name="tvp", bufs=4))
             up = p2.enter_context(tc.tile_pool(name="up", bufs=5))
             bp = p2.enter_context(tc.tile_pool(name="bp", bufs=4))
             pp = p2.enter_context(tc.tile_pool(name="pp", bufs=8))
-            obp = p2.enter_context(tc.tile_pool(name="obp", bufs=4))
+            obp = p2.enter_context(tc.tile_pool(name="obp", bufs=8))
 
             zh = z_bufs[NZ]
             u_tiles = {}
-            three = {}
             turned = {}
             pair = {}
 
             def relu(out_ap, in_ap, f, a, b):
                 nc.scalar.activation(out=out_ap, in_=in_ap, func=ACT.Relu, bias=b[:, f : f + 1], scale=a[:, f : f + 1])
-
-            def mains(zb, f):
-                return zb[:, f, 0 : 2 * EV].rearrange("p (s t x) -> p t s x", s=2, x=RS)[:, :, :, 4:P]
-
-            def borders(zb, f):
-                return zb[:, f, P : P + 2 * (RS + 4)].rearrange("p (s g x) -> p g s x", s=2, x=4)[:, 0 : RS // 4 + 1 : RS // 4, :, :]
 
             def norm_relu(j, f):
                 zb = z_bufs[j % NZ]
@@ -319,24 +306,29 @@ def tile_graphconvolutionbatch_kernel(tc, H_bytes, H_scale, W, gamma, beta, out)
                 else:
                     y = py.tile([P, 512], F32, name="y")
                 mx_features(y, f, j * 512)
-                src = y[:].rearrange("p (t x) -> p t x", t=TB)
-                src_main = src[:, :, 0 : 2 * MAIN].rearrange("p t (s x) -> p t s x", s=2)
-                src_border = src[:, :, 2 * MAIN : 2 * P].rearrange("p t (s x) -> p t s x", s=2)
+                src = y[:].rearrange("p (t s x) -> p t s x", t=TB, s=2)
+                dst = runs(zb)[:, f, :, :, 4:RS].rearrange("p s t x -> p t s x")
                 if j == NB - 1:
-                    for t, main, border in ((0, (a9, b9), (a6, b6)), (1, (a6, b6), (a4, b4))):
-                        relu(mains(zb, f)[:, t, :, :], src_main[:, t, :, :], f, *main)
-                        relu(borders(zb, f)[:, t, :, :], src_border[:, t, :, :], f, *border)
+                    relu(dst[:, 0, :, :], src[:, 0, :, :], f, a9, b9)
+                    relu(dst[:, 1, :, :], src[:, 1, :, :], f, a6, b6)
                 else:
-                    relu(mains(zb, f), src_main, f, a9, b9)
-                    relu(borders(zb, f), src_border, f, a6, b6)
+                    relu(dst, src, f, a9, b9)
 
             def swap_columns(f):
-                def both(zb):
-                    return zb[:, f, 4 : 4 + 2 * (EV - 4)].rearrange("p (s y) -> p s y", s=2)[:, :, 0:P].rearrange(
-                        "p s (x h) -> p s x h", h=2
-                    )
+                def first(zb):
+                    return runs(zb)[:, f, :, 0, 4:RS].rearrange("p s (x h) -> p s x h", h=2)
 
-                nc.vector.tensor_copy(out=both(zh), in_=both(z_bufs[0])[:, :, :, ::-1])
+                nc.vector.tensor_copy(out=first(zh), in_=first(z_bufs[0])[:, :, :, ::-1])
+
+            def weigh(engine, j, f0, f1):
+                zb = zh if j < 0 else z_bufs[j % NZ]
+                ends = zb[:, f0:f1, P : P + 4 * RS].rearrange("p f (k x) -> p f k x", x=RS)[:, :, :, 0:4]
+                if j == NB - 1:
+                    parts = ((ends[:, :, 0::2, :], RHO), (ends[:, :, 1::2, :], RHO * KAPPA))
+                else:
+                    parts = ((ends, RHO),)
+                for cells, weight in parts:
+                    engine.tensor_scalar(out=cells, in0=cells, scalar1=weight, scalar2=0.0, op0=ALU.mult, op1=ALU.add)
 
             def two_rows(engine, j, f0, f1):
                 if j not in u_tiles:
@@ -346,22 +338,8 @@ def tile_graphconvolutionbatch_kernel(tc, H_bytes, H_scale, W, gamma, beta, out)
                 n = 1 if j < 0 else TB
                 engine.tensor_tensor(
                     out=u_tiles[j][:, f0:f1, 0:n, :],
-                    in0=even(zb)[:, f0:f1, 0:n, 0:P],
-                    in1=odd(zb)[:, f0:f1, 0:n, 4:RS],
-                    op=ALU.add,
-                )
-
-            def three_rows(engine, j):
-                zb = zh if j < 0 else z_bufs[j % NZ]
-                n = 1 if j < 0 else TB
-                tv = tvp.tile([P, 2, TB, P], F32, name="tv")
-                three[j] = tv
-                engine.tensor_tensor(
-                    out=tv[:, :, 0:n, :],
-                    in0=u_tiles[j][:, 0, 0:n, :].unsqueeze(1).to_broadcast([P, 2, n, P]),
-                    in1=zb[:, 0, 0 : 2 * (EV + 4)].rearrange("p (s y) -> p s y", s=2)[:, :, 0:EV].rearrange(
-                        "p s (t x) -> p s t x", x=RS
-                    )[:, :, 0:n, 0:P],
+                    in0=runs(zb)[:, f0:f1, 1, 0:n, 4:RS],
+                    in1=runs(zb)[:, f0:f1, 0, 0:n, 4:RS],
                     op=ALU.add,
                 )
 
@@ -376,19 +354,15 @@ def tile_graphconvolutionbatch_kernel(tc, H_bytes, H_scale, W, gamma, beta, out)
                 else:
                     o = po.tile([P, NF], F32, name="turned_odd")
                 for f in range(FC):
-                    w0 = EV + 4 if e else 0
-                    if f == 0:
-                        wins = [three[j][:, e, tt, :]]
-                    else:
-                        wins = [u_tiles[j][:, f, tt, :], zb[:, f, w0 + tt * RS : w0 + tt * RS + P]]
-                    for w, win in enumerate(wins):
+                    w0 = EV + 8 if e else 0
+                    for w, win in enumerate((u_tiles[j][:, f, tt, :], zb[:, f, w0 + tt * RS : w0 + tt * RS + P])):
                         nc.tensor.matmul(
                             out=o[:, f * P : (f + 1) * P],
                             lhsT=win,
                             rhs=ident[:],
                             is_transpose=True,
                             start=(w == 0),
-                            stop=(w == len(wins) - 1),
+                            stop=(w == 1),
                         )
                 turned[t, e] = o
 
@@ -411,11 +385,13 @@ def tile_graphconvolutionbatch_kernel(tc, H_bytes, H_scale, W, gamma, beta, out)
 
             for f in range(FC):
                 norm_relu(0, f)
-                two_rows(nc.vector, 0, f, f + 1)
+                weigh(nc.vector, 0, f, f + 1)
+                if f > 0:
+                    two_rows(nc.vector, 0, f - 1, f)
+            two_rows(nc.vector, 0, FC - 1, FC)
+            for f in range(FC):
                 swap_columns(f)
             two_rows(nc.vector, -1, 0, FC)
-            three_rows(nc.vector, 0)
-            three_rows(nc.vector, -1)
             norm_relu(1, 0)
             norm_relu(1, 1)
             for q in range(NB):
@@ -427,14 +403,20 @@ def tile_graphconvolutionbatch_kernel(tc, H_bytes, H_scale, W, gamma, beta, out)
                     norm_relu(q + 2, 0)
                     norm_relu(q + 2, 1)
                 if q + 1 < NB:
-                    two_rows(nc.gpsimd, q + 1, 0, FC)
-                    three_rows(nc.gpsimd, q + 1)
+                    adder = nc.vector if q == 0 else nc.gpsimd
+                    for f0 in (0, 2) if q + 1 == NB - 1 else (0,):
+                        f1 = f0 + 2 if q + 1 == NB - 1 else FC
+                        weigh(adder, q + 1, f0, f1)
+                        two_rows(adder, q + 1, f0, f1)
                 for e in range(2):
                     turn_out(TB * q, e)
                 both = {}
                 for e in range(2):
                     bt = bp.tile([P, NF], F32, name="bt")
-                    nc.scalar.activation(out=bt[:], in_=turned[TB * q, e][:], func=ACT.Copy, scale=dcol[:, e : e + 1])
+                    if e == 0:
+                        nc.scalar.activation(out=bt[:], in_=turned[TB * q, e][:], func=ACT.Copy, scale=dcol[:, e : e + 1])
+                    else:
+                        nc.vector.tensor_scalar(out=bt[:], in0=turned[TB * q, e][:], scalar1=dcol[:, e : e + 1], scalar2=None, op0=ALU.mult)
                     both[e] = bt
                 if q > 0:
                     for e in range(2):
@@ -463,6 +445,8 @@ def tile_graphconvolutionbatch_kernel(tc, H_bytes, H_scale, W, gamma, beta, out)
                     last = obp.tile([P, 2, TB, NF], F32, name="ob")
                     for e in range(2):
                         nc.scalar.activation(out=last[:, e, 0, :], in_=pair[q, e][:], func=ACT.Copy, scale=fac[:, e : e + 1])
+                if q == NB - 1:
+                    ob = obp.tile([P, 2, TB, NF], F32, name="ob")
                 if q > 0:
                     for e in range(2):
                         add_turned(ob[:, e, 1, :], TB * q - 1, e, pair[q, e][:])

@@ -24,7 +24,7 @@ IB = P // 2
 RUN = TB * P
 RS = P + 4
 EV = P + TB * RS - 4
-ZR = 2 * EV
+ZR = 2 * EV + 16
 NZ = 4
 FS = FC - 1
 EPS_BN = 1e-5
@@ -108,7 +108,7 @@ def tile_graphconvolutionbatch_kernel(tc, H_bytes, H_scale, W, gamma, beta, out)
 
             for zb in z_bufs:
                 nc.vector.memset(runs(zb)[:, :, :, :, 0:4], 0.0)
-                nc.vector.memset(zb[:, :, EV + TB * RS : ZR], 0.0)
+                nc.vector.memset(zb[:, :, EV + TB * RS : EV + TB * RS + 4], 0.0)
             nc.gpsimd.memset(warm[:, 0:1], 1.0)
             nc.scalar.activation(out=warm[:, 1:2], in_=warm[:, 0:1], func=ACT.Abs_reciprocal_sqrt)
             make_identity(nc, ident[:])
@@ -168,8 +168,8 @@ def tile_graphconvolutionbatch_kernel(tc, H_bytes, H_scale, W, gamma, beta, out)
                                 xt[:, h, u, :], words[:, cl * (K // 2) + u : (cl + 1) * (K // 2) : 2], perm[:]
                             )
                     nc.scalar.copy(
-                        out=gw[:, tt * K : (tt + 1) * K].rearrange("p (r x) -> p r x", x=4),
-                        in_=xt[:].rearrange("p h u r -> p r (h u)"),
+                        out=gw.rearrange("p (h t r u) -> p t h r u", h=2, t=TB, u=2)[:, tt, :, :, :],
+                        in_=xt[:].rearrange("p h u r -> p h r u"),
                     )
                 grouped[j] = g
 
@@ -286,6 +286,7 @@ def tile_graphconvolutionbatch_kernel(tc, H_bytes, H_scale, W, gamma, beta, out)
         with ExitStack() as p2:
             pe = p2.enter_context(tc.psum_pool(name="pe", bufs=2))
             po = p2.enter_context(tc.psum_pool(name="po", bufs=4))
+            tvp = p2.enter_context(tc.tile_pool(name="tvp", bufs=5))
             up = p2.enter_context(tc.tile_pool(name="up", bufs=5))
             bp = p2.enter_context(tc.tile_pool(name="bp", bufs=4))
             pp = p2.enter_context(tc.tile_pool(name="pp", bufs=8))
@@ -293,6 +294,7 @@ def tile_graphconvolutionbatch_kernel(tc, H_bytes, H_scale, W, gamma, beta, out)
 
             zh = z_bufs[NZ]
             u_tiles = {}
+            three = {}
             turned = {}
             pair = {}
 
@@ -306,11 +308,11 @@ def tile_graphconvolutionbatch_kernel(tc, H_bytes, H_scale, W, gamma, beta, out)
                 else:
                     y = py.tile([P, 512], F32, name="y")
                 mx_features(y, f, j * 512)
-                src = y[:].rearrange("p (t s x) -> p t s x", t=TB, s=2)
-                dst = runs(zb)[:, f, :, :, 4:RS].rearrange("p s t x -> p t s x")
+                src = y[:].rearrange("p (h t s x) -> p t s x h", h=2, t=TB, s=2)
+                dst = runs(zb)[:, f, :, :, 4:RS].rearrange("p s t (x h) -> p t s x h", h=2)
                 if j == NB - 1:
-                    relu(dst[:, 0, :, :], src[:, 0, :, :], f, a9, b9)
-                    relu(dst[:, 1, :, :], src[:, 1, :, :], f, a6, b6)
+                    relu(dst[:, 0, :, :, :], src[:, 0, :, :, :], f, a9, b9)
+                    relu(dst[:, 1, :, :, :], src[:, 1, :, :, :], f, a6, b6)
                 else:
                     relu(dst, src, f, a9, b9)
 
@@ -343,6 +345,23 @@ def tile_graphconvolutionbatch_kernel(tc, H_bytes, H_scale, W, gamma, beta, out)
                     op=ALU.add,
                 )
 
+            def three_rows(engine, j):
+                zb = zh if j < 0 else z_bufs[j % NZ]
+                n = 1 if j < 0 else TB
+                tv = tvp.tile([P, 2, TB, P], F32, name="tv")
+                three[j] = tv
+                engine.tensor_tensor(
+                    out=tv[:, :, 0:n, :],
+                    in0=u_tiles[j][:, 0, 0:n, :].unsqueeze(1).to_broadcast([P, 2, n, P]),
+                    in1=windows(zb, n),
+                    op=ALU.add,
+                )
+
+            def windows(zb, n):
+                return zb[:, 0, 0 : 2 * (EV + 8)].rearrange("p (s y) -> p s y", s=2)[:, :, 0 : TB * RS].rearrange(
+                    "p s (t x) -> p s t x", x=RS
+                )[:, :, 0:n, 0:P]
+
             def turn_out(t, e):
                 j = -1 if t < 0 else t // TB
                 tt = 0 if t < 0 else t % TB
@@ -355,14 +374,18 @@ def tile_graphconvolutionbatch_kernel(tc, H_bytes, H_scale, W, gamma, beta, out)
                     o = po.tile([P, NF], F32, name="turned_odd")
                 for f in range(FC):
                     w0 = EV + 8 if e else 0
-                    for w, win in enumerate((u_tiles[j][:, f, tt, :], zb[:, f, w0 + tt * RS : w0 + tt * RS + P])):
+                    if f == 0:
+                        wins = [three[j][:, e, tt, :]]
+                    else:
+                        wins = [u_tiles[j][:, f, tt, :], zb[:, f, w0 + tt * RS : w0 + tt * RS + P]]
+                    for w, win in enumerate(wins):
                         nc.tensor.matmul(
                             out=o[:, f * P : (f + 1) * P],
                             lhsT=win,
                             rhs=ident[:],
                             is_transpose=True,
                             start=(w == 0),
-                            stop=(w == 1),
+                            stop=(w == len(wins) - 1),
                         )
                 turned[t, e] = o
 
@@ -389,9 +412,11 @@ def tile_graphconvolutionbatch_kernel(tc, H_bytes, H_scale, W, gamma, beta, out)
                 if f > 0:
                     two_rows(nc.vector, 0, f - 1, f)
             two_rows(nc.vector, 0, FC - 1, FC)
+            three_rows(nc.vector, 0)
             for f in range(FC):
                 swap_columns(f)
             two_rows(nc.vector, -1, 0, FC)
+            three_rows(nc.vector, -1)
             norm_relu(1, 0)
             norm_relu(1, 1)
             for q in range(NB):
@@ -413,10 +438,7 @@ def tile_graphconvolutionbatch_kernel(tc, H_bytes, H_scale, W, gamma, beta, out)
                 both = {}
                 for e in range(2):
                     bt = bp.tile([P, NF], F32, name="bt")
-                    if e == 0:
-                        nc.scalar.activation(out=bt[:], in_=turned[TB * q, e][:], func=ACT.Copy, scale=dcol[:, e : e + 1])
-                    else:
-                        nc.vector.tensor_scalar(out=bt[:], in0=turned[TB * q, e][:], scalar1=dcol[:, e : e + 1], scalar2=None, op0=ALU.mult)
+                    nc.scalar.activation(out=bt[:], in_=turned[TB * q, e][:], func=ACT.Copy, scale=dcol[:, e : e + 1])
                     both[e] = bt
                 if q > 0:
                     for e in range(2):
@@ -437,6 +459,8 @@ def tile_graphconvolutionbatch_kernel(tc, H_bytes, H_scale, W, gamma, beta, out)
                 if q == 1:
                     for e in range(2):
                         turn_out(-1, e)
+                if q + 1 < NB:
+                    three_rows(nc.vector, q + 1)
                 for e in range(2):
                     pr = pp.tile([P, NF], F32, name="pr")
                     add_turned(pr[:], TB * q + 1, e, both[e][:])

@@ -54,7 +54,6 @@ def tile_graphconvolutionbatch_kernel(tc, H_bytes, H_scale, W, gamma, beta, out)
         b9 = keep.tile([P, FC], F32)
         a6 = keep.tile([P, FC], F32)
         b6 = keep.tile([P, FC], F32)
-        dcol = keep.tile([P, 2], F32)
         fac = keep.tile([P, 2], F32)
         z_bufs = []
         for i in range(NZ + 1):
@@ -106,9 +105,6 @@ def tile_graphconvolutionbatch_kernel(tc, H_bytes, H_scale, W, gamma, beta, out)
                 nc.sync.dma_start(out=gam_bf[:], in_=gamma.rearrange("(c p) -> p c", p=P))
                 nc.sync.dma_start(out=bet_bf[:], in_=beta.rearrange("(c p) -> p c", p=P))
 
-            for zb in z_bufs:
-                nc.vector.memset(runs(zb)[:, :, :, :, 0:4], 0.0)
-                nc.vector.memset(zb[:, :, EV + TB * RS : EV + TB * RS + 4], 0.0)
             nc.gpsimd.memset(warm[:, 0:1], 1.0)
             nc.scalar.activation(out=warm[:, 1:2], in_=warm[:, 0:1], func=ACT.Abs_reciprocal_sqrt)
             make_identity(nc, ident[:])
@@ -130,8 +126,8 @@ def tile_graphconvolutionbatch_kernel(tc, H_bytes, H_scale, W, gamma, beta, out)
             grouped = {}
 
             def small_constants():
-                nc.vector.tensor_scalar(out=g9[:], in0=gam_bf[:], scalar1=D9, scalar2=None, op0=ALU.mult)
-                nc.vector.tensor_scalar(out=bet9[:], in0=bet_bf[:], scalar1=D9, scalar2=None, op0=ALU.mult)
+                nc.vector.tensor_scalar(out=g9[:], in0=gam_bf[:], scalar1=D9 * D9, scalar2=None, op0=ALU.mult)
+                nc.vector.tensor_scalar(out=bet9[:], in0=bet_bf[:], scalar1=D9 * D9, scalar2=None, op0=ALU.mult)
                 for e in range(2):
                     nc.vector.tensor_reduce(
                         out=edge[:, e : e + 1],
@@ -139,7 +135,6 @@ def tile_graphconvolutionbatch_kernel(tc, H_bytes, H_scale, W, gamma, beta, out)
                         axis=AX.X,
                         op=ALU.add,
                     )
-                nc.vector.tensor_scalar(out=dcol[:], in0=edge[:], scalar1=D6 - D9, scalar2=D9, op0=ALU.mult, op1=ALU.add)
                 nc.vector.tensor_scalar(out=fac[:], in0=edge[:], scalar1=D4 / D6 - RHO, scalar2=RHO, op0=ALU.mult, op1=ALU.add)
 
             def widen(j):
@@ -330,7 +325,10 @@ def tile_graphconvolutionbatch_kernel(tc, H_bytes, H_scale, W, gamma, beta, out)
                 else:
                     parts = ((ends, RHO),)
                 for cells, weight in parts:
-                    engine.tensor_scalar(out=cells, in0=cells, scalar1=weight, scalar2=0.0, op0=ALU.mult, op1=ALU.add)
+                    if engine is nc.scalar:
+                        nc.scalar.activation(out=cells, in_=cells, func=ACT.Copy, scale=weight)
+                    else:
+                        engine.tensor_scalar(out=cells, in0=cells, scalar1=weight, scalar2=0.0, op0=ALU.mult, op1=ALU.add)
 
             def two_rows(engine, j, f0, f1):
                 if j not in u_tiles:
@@ -344,6 +342,18 @@ def tile_graphconvolutionbatch_kernel(tc, H_bytes, H_scale, W, gamma, beta, out)
                     in1=runs(zb)[:, f0:f1, 0, 0:n, 4:RS],
                     op=ALU.add,
                 )
+
+            def border_rows(j):
+                zb = zh if j < 0 else z_bufs[j % NZ]
+                n = 1 if j < 0 else TB
+                for at, lo in ((0, 0), (EV + RS, P - 4)):
+                    nc.vector.tensor_scalar(
+                        out=zb[:, :, at : at + TB * RS].rearrange("p f (t x) -> p f t x", x=RS)[:, :, 0:n, 0:4],
+                        in0=u_tiles[j][:, :, 0:n, lo : lo + 4],
+                        scalar1=RHO - 1.0,
+                        scalar2=None,
+                        op0=ALU.mult,
+                    )
 
             def three_rows(engine, j):
                 zb = zh if j < 0 else z_bufs[j % NZ]
@@ -372,27 +382,23 @@ def tile_graphconvolutionbatch_kernel(tc, H_bytes, H_scale, W, gamma, beta, out)
                     o = pe.tile([P, NF], F32, name="turned_even")
                 else:
                     o = po.tile([P, NF], F32, name="turned_odd")
-                for f in range(FC):
-                    w0 = EV + 8 if e else 0
-                    if f == 0:
-                        wins = [three[j][:, e, tt, :]]
-                    else:
-                        wins = [u_tiles[j][:, f, tt, :], zb[:, f, w0 + tt * RS : w0 + tt * RS + P]]
-                    for w, win in enumerate(wins):
-                        nc.tensor.matmul(
-                            out=o[:, f * P : (f + 1) * P],
-                            lhsT=win,
-                            rhs=ident[:],
-                            is_transpose=True,
-                            start=(w == 0),
-                            stop=(w == len(wins) - 1),
-                        )
+                w0 = (EV + 8 if e else 0) + tt * RS
+                wins = [(f, u_tiles[j][:, f, tt, :]) for f in range(1, FC)]
+                wins.append((0, three[j][:, e, tt, :]))
+                wins.extend((f, zb[:, f, w0 : w0 + P]) for f in range(1, FC))
+                for w, (f, win) in enumerate(wins):
+                    nc.tensor.matmul(
+                        out=o[:, f * P : (f + 1) * P],
+                        lhsT=win,
+                        rhs=ident[:],
+                        is_transpose=True,
+                        start=(w == 0),
+                        stop=(w == len(wins) - 1),
+                    )
                 turned[t, e] = o
 
             def add_turned(dst, t, e, other):
-                nc.vector.scalar_tensor_tensor(
-                    out=dst, in0=turned[t, e][:], scalar=dcol[:, e : e + 1], in1=other, op0=ALU.mult, op1=ALU.add
-                )
+                nc.vector.tensor_tensor(out=dst, in0=turned[t, e][:], in1=other, op=ALU.add)
 
             out_v = out.rearrange("b (i e c) f -> b c i e f", e=2, c=COLS)
             out_c = out.rearrange("b (i e c) f -> b i e (c f)", e=2, c=COLS)
@@ -412,10 +418,12 @@ def tile_graphconvolutionbatch_kernel(tc, H_bytes, H_scale, W, gamma, beta, out)
                 if f > 0:
                     two_rows(nc.vector, 0, f - 1, f)
             two_rows(nc.vector, 0, FC - 1, FC)
+            border_rows(0)
             three_rows(nc.vector, 0)
             for f in range(FC):
                 swap_columns(f)
             two_rows(nc.vector, -1, 0, FC)
+            border_rows(-1)
             three_rows(nc.vector, -1)
             norm_relu(1, 0)
             norm_relu(1, 1)
@@ -431,14 +439,15 @@ def tile_graphconvolutionbatch_kernel(tc, H_bytes, H_scale, W, gamma, beta, out)
                     adder = nc.vector if q == 0 else nc.gpsimd
                     for f0 in (0, 2) if q + 1 == NB - 1 else (0,):
                         f1 = f0 + 2 if q + 1 == NB - 1 else FC
-                        weigh(adder, q + 1, f0, f1)
+                        if q == 0:
+                            weigh(nc.vector, 1, 0, FC)
                         two_rows(adder, q + 1, f0, f1)
                 for e in range(2):
                     turn_out(TB * q, e)
                 both = {}
                 for e in range(2):
                     bt = bp.tile([P, NF], F32, name="bt")
-                    nc.scalar.activation(out=bt[:], in_=turned[TB * q, e][:], func=ACT.Copy, scale=dcol[:, e : e + 1])
+                    nc.scalar.copy(out=bt[:], in_=turned[TB * q, e][:])
                     both[e] = bt
                 if q > 0:
                     for e in range(2):
@@ -451,18 +460,22 @@ def tile_graphconvolutionbatch_kernel(tc, H_bytes, H_scale, W, gamma, beta, out)
                 elif q + 2 < NB:
                     norm_relu(q + 2, 2)
                     norm_relu(q + 2, 3)
+                    weigh(nc.scalar, q + 2, 0, FC)
                 for e in range(2):
                     turn_out(TB * q + 1, e)
                 if q == 0:
                     norm_relu(2, 2)
                     norm_relu(2, 3)
+                    weigh(nc.scalar, 2, 0, FC)
                 if q == 1:
                     for e in range(2):
                         turn_out(-1, e)
                 if q + 1 < NB:
-                    three_rows(nc.vector, q + 1)
+                    border_rows(q + 1)
                 for e in range(2):
                     pr = pp.tile([P, NF], F32, name="pr")
+                    if e == 1 and q + 1 < NB:
+                        three_rows(nc.vector, q + 1)
                     add_turned(pr[:], TB * q + 1, e, both[e][:])
                     pair[q, e] = pr
                 if q == NB - 1:

@@ -146,6 +146,15 @@ def tile_graphconvolutionbatch_kernel(tc, H_bytes, H_scale, W, gamma, beta, out)
                         nc.vector.tensor_tensor(
                             out=hw[:, cols], in0=hb[:, cols].bitcast(FP8), in1=sb4[:, 0:K], op=ALU.mult
                         )
+                elif j == NB - 1:
+                    nc.vector.tensor_tensor(
+                        out=hw[:, K : 3 * K], in0=hb[:, K : 3 * K].bitcast(FP8), in1=sb4[:, K : 3 * K], op=ALU.mult
+                    )
+                    for cl in (0, 3):
+                        cols = slice(cl * K, (cl + 1) * K)
+                        nc.vector.tensor_tensor(
+                            out=hw[:, cols], in0=hb[:, cols].bitcast(FP8), in1=sb4[:, 0:K], op=ALU.mult
+                        )
                 else:
                     nc.vector.tensor_tensor(out=hw[:], in0=hb[:].bitcast(FP8), in1=sb4[:], op=ALU.mult)
                 widened[j] = hw
@@ -300,6 +309,8 @@ def tile_graphconvolutionbatch_kernel(tc, H_bytes, H_scale, W, gamma, beta, out)
                 zb = z_bufs[j % NZ]
                 if j == 0:
                     y = po.tile([P, NF], F32, name="turned_odd")
+                elif j == 1 and f < 2:
+                    y = pe.tile([P, NF], F32, name="turned_even")
                 else:
                     y = py.tile([P, 512], F32, name="y")
                 mx_features(y, f, j * 512)
@@ -472,10 +483,9 @@ def tile_graphconvolutionbatch_kernel(tc, H_bytes, H_scale, W, gamma, beta, out)
                         turn_out(-1, e)
                 if q + 1 < NB:
                     border_rows(q + 1)
+                    three_rows(nc.vector, q + 1)
                 for e in range(2):
                     pr = pp.tile([P, NF], F32, name="pr")
-                    if e == 1 and q + 1 < NB:
-                        three_rows(nc.vector, q + 1)
                     add_turned(pr[:], TB * q + 1, e, both[e][:])
                     pair[q, e] = pr
                 if q == NB - 1:

@@ -394,9 +394,11 @@ def tile_graphconvolutionbatch_kernel(tc, H_bytes, H_scale, W, gamma, beta, out)
                 else:
                     o = po.tile([P, NF], F32, name="turned_odd")
                 w0 = (EV + 8 if e else 0) + tt * RS
-                wins = [(f, u_tiles[j][:, f, tt, :]) for f in range(1, FC)]
-                wins.append((0, three[j][:, e, tt, :]))
-                wins.extend((f, zb[:, f, w0 : w0 + P]) for f in range(1, FC))
+                f0 = 1 if j in three else 0
+                wins = [(f, u_tiles[j][:, f, tt, :]) for f in range(f0, FC)]
+                if j in three:
+                    wins.append((0, three[j][:, e, tt, :]))
+                wins.extend((f, zb[:, f, w0 : w0 + P]) for f in range(f0, FC))
                 for w, (f, win) in enumerate(wins):
                     nc.tensor.matmul(
                         out=o[:, f * P : (f + 1) * P],
@@ -430,22 +432,27 @@ def tile_graphconvolutionbatch_kernel(tc, H_bytes, H_scale, W, gamma, beta, out)
                     two_rows(nc.vector, 0, f - 1, f)
             two_rows(nc.vector, 0, FC - 1, FC)
             border_rows(0)
-            three_rows(nc.vector, 0)
             for f in range(FC):
                 swap_columns(f)
             two_rows(nc.vector, -1, 0, FC)
             border_rows(-1)
-            three_rows(nc.vector, -1)
-            norm_relu(1, 0)
-            norm_relu(1, 1)
+            pairs = [(j, a) for j in range(1, NB) for a in range(2)]
+            done = [0]
+
+            def relus_up_to(n):
+                while done[0] < min(n, len(pairs)):
+                    j, a = pairs[done[0]]
+                    norm_relu(j, 2 * a)
+                    norm_relu(j, 2 * a + 1)
+                    if a == 1 and j > 1:
+                        weigh(nc.scalar, j, 0, FC)
+                    done[0] += 1
+
             for q in range(NB):
                 ob = obp.tile([P, 2, TB, NF], F32, name="ob")
-                if q == 0:
-                    norm_relu(1, 2)
-                    norm_relu(1, 3)
-                elif q + 2 < NB:
-                    norm_relu(q + 2, 0)
-                    norm_relu(q + 2, 1)
+                before = [2]
+                between = [3]
+                relus_up_to(before[q] if q < len(before) else 2 * q + 3)
                 if q + 1 < NB:
                     adder = nc.vector if q == 0 else nc.gpsimd
                     for f0 in (0, 2) if q + 1 == NB - 1 else (0,):
@@ -453,6 +460,10 @@ def tile_graphconvolutionbatch_kernel(tc, H_bytes, H_scale, W, gamma, beta, out)
                         if q == 0:
                             weigh(nc.vector, 1, 0, FC)
                         two_rows(adder, q + 1, f0, f1)
+                if q == 0:
+                    idle = po.tile([P, NF], F32, name="turned_odd")
+                    for f in range(6):
+                        mx_features(idle, f % FC, 0)
                 for e in range(2):
                     turn_out(TB * q, e)
                 both = {}
@@ -465,25 +476,16 @@ def tile_graphconvolutionbatch_kernel(tc, H_bytes, H_scale, W, gamma, beta, out)
                         add_turned(ob[:, e, 0, :], TB * q, e, pair[q - 1, e][:])
                 if q == NB - 1:
                     store(ob, 0, TB * q - 1, 1)
-                if q == 0:
-                    norm_relu(2, 0)
-                    norm_relu(2, 1)
-                elif q + 2 < NB:
-                    norm_relu(q + 2, 2)
-                    norm_relu(q + 2, 3)
-                    weigh(nc.scalar, q + 2, 0, FC)
+                relus_up_to(between[q] if q < len(between) else 2 * q + 4)
                 for e in range(2):
                     turn_out(TB * q + 1, e)
-                if q == 0:
-                    norm_relu(2, 2)
-                    norm_relu(2, 3)
-                    weigh(nc.scalar, 2, 0, FC)
                 if q == 1:
                     for e in range(2):
                         turn_out(-1, e)
                 if q + 1 < NB:
                     border_rows(q + 1)
-                    three_rows(nc.vector, q + 1)
+                    if 0 < q < NB - 2 - 1:
+                        three_rows(nc.vector, q + 1)
                 for e in range(2):
                     pr = pp.tile([P, NF], F32, name="pr")
                     add_turned(pr[:], TB * q + 1, e, both[e][:])

from contextlib import ExitStack

import concourse.mybir as mybir
from concourse.masks import make_identity

F32 = mybir.dt.float32
BF16 = mybir.dt.bfloat16
U32 = mybir.dt.uint32
U8 = mybir.dt.uint8
FP8 = mybir.dt.float8_e4m3fn
FP8X4 = mybir.dt.float8_e4m3fn_x4
ALU = mybir.AluOpType
ACT = mybir.ActivationFunctionType
AX = mybir.AxisListType

P = 128
BATCH, ROWS, COLS, K, NF = 2, 64, 64, 512, 512
NODES = BATCH * ROWS * COLS
FC = NF // P
TB = 2
NT = COLS // 2
NB = NT // TB
IB = P // 2
RUN = TB * P
RS = P + 4
EV = P + TB * RS - 4
ZR = 2 * EV + 16
NZ = 4
FS = FC - 1
EPS_BN = 1e-5
D9 = (9.0 + 1e-5) ** -0.5
D6 = (6.0 + 1e-5) ** -0.5
D4 = (4.0 + 1e-5) ** -0.5
RHO = D6 / D9
KAPPA = (D4 / D9) / (RHO * RHO)

FLOPS = 2 * NODES * K * NF


def tile_graphconvolutionbatch_kernel(tc, H_bytes, H_scale, W, gamma, beta, out):
    nc = tc.nc
    with ExitStack() as ctx:
        keep = ctx.enter_context(tc.tile_pool(name="keep", bufs=1))
        py = ctx.enter_context(tc.psum_pool(name="py", bufs=2))
        ctx.enter_context(tc.manual_schedule())
        ident = keep.tile([P, P], F32)
        perm = keep.tile([P, P], F32)
        w_codes = keep.tile([P, NF], U32, align_bytes=64)
        w_sc = keep.tile([P, NF], U8, align_bytes=64)
        codes = keep.tile([P, NODES], U32, align_bytes=64)
        hsc = keep.tile([P, NODES], U8, align_bytes=64)
        ssq = keep.tile([P, FC, NB], F32)
        a9 = keep.tile([P, FC], F32)
        b9 = keep.tile([P, FC], F32)
        a6 = keep.tile([P, FC], F32)
        b6 = keep.tile([P, FC], F32)
        fac = keep.tile([P, 2], F32)
        z_bufs = []
        for i in range(NZ + 1):
            zb = keep.tile([P, FC, ZR], F32, name="z_buf%d" % i)
            z_bufs.append(zb)

        def runs(zb):
            return zb[:, :, 0 : 2 * EV].rearrange("p f (s y) -> p f s y", s=2)[:, :, :, 0 : TB * RS].rearrange(
                "p f s (t x) -> p f s t x", x=RS
            )

        def mx_features(y, f, n0):
            nc.tensor.matmul_mx(
                out=y[:],
                lhsT=w_codes[:, f * P : (f + 1) * P].bitcast(FP8X4),
                lhsT_scale=w_sc[:, f * P : (f + 1) * P],
                rhs=codes[:, n0 : n0 + 512].bitcast(FP8X4),
                rhs_scale=hsc[:, n0 : n0 + 512],
                start=True,
                stop=True,
            )

        with ExitStack() as p1:
            pt = p1.enter_context(tc.psum_pool(name="pt", bufs=3))
            py1 = p1.enter_context(tc.psum_pool(name="py1", bufs=2))
            pm = p1.enter_context(tc.psum_pool(name="pm", bufs=1))
            one = p1.enter_context(tc.tile_pool(name="one", bufs=1))
            hbp = p1.enter_context(tc.tile_pool(name="hbp", bufs=NB))
            hwp = p1.enter_context(tc.tile_pool(name="hwp", bufs=3))
            gp = p1.enter_context(tc.tile_pool(name="gp", bufs=3))
            jp = p1.enter_context(tc.tile_pool(name="jp", bufs=2))

            sb4 = one.tile([P, 4 * K], F32)
            nc.sync.dma_start(out=sb4[:, 0:K], in_=H_scale.rearrange("a b k -> (a b k)").partition_broadcast(P))
            hv = H_bytes.rearrange("b (r c) k -> (b r) (c k)", c=COLS)
            h_bytes_sb = []
            w_raw = one.tile([P, 4, NF], BF16)
            warm = one.tile([P, 2], F32)
            for j in range(NB):
                hb = hbp.tile([P, 4 * K], U8, name="h_bytes_tile")
                for h, c0 in enumerate((30 - 2 * j, 32 + 2 * j)):
                    nc.sync.dma_start(out=hb[:, h * 2 * K : (h + 1) * 2 * K], in_=hv[:, c0 * K : (c0 + 2) * K])
                h_bytes_sb.append(hb)
                if j == 0:
                    nc.sync.dma_start(out=w_raw[:], in_=W.rearrange("(p j) n -> p j n", j=4))
            gam_bf = one.tile([P, FC], BF16)
            bet_bf = one.tile([P, FC], BF16)
            with nc.allow_non_contiguous_dma(reason="512 values, one to a partition and chunk"):
                nc.sync.dma_start(out=gam_bf[:], in_=gamma.rearrange("(c p) -> p c", p=P))
                nc.sync.dma_start(out=bet_bf[:], in_=beta.rearrange("(c p) -> p c", p=P))

            nc.gpsimd.memset(warm[:, 0:1], 1.0)
            nc.scalar.activation(out=warm[:, 1:2], in_=warm[:, 0:1], func=ACT.Abs_reciprocal_sqrt)
            make_identity(nc, ident[:])
            for s in range(2):
                nc.vector.tensor_copy(
                    out=perm[:, s * IB : (s + 1) * IB].rearrange("p (i b) -> p i b", b=BATCH),
                    in_=ident[:].rearrange("p (b i t) -> p t i b", b=BATCH, t=2)[:, 1 - s, :, :],
                )
            nc.scalar.copy(out=sb4[:, K : 2 * K], in_=sb4[:, 0:K])
            nc.scalar.copy(out=sb4[:, 2 * K : 4 * K], in_=sb4[:, 0 : 2 * K])
            w_grp = one.tile([P, NF, 4], BF16, align_bytes=64)
            nc.scalar.copy(out=w_grp[:], in_=w_raw[:].rearrange("p j n -> p n j"))
            g9 = one.tile([P, FC], F32)
            bet9 = one.tile([P, FC], F32)
            edge = one.tile([P, 2], F32)

            colsum = pm.tile([P, NF], F32, name="colsum")
            widened = {}
            grouped = {}

            def small_constants():
                nc.vector.tensor_scalar(out=g9[:], in0=gam_bf[:], scalar1=D9 * D9, scalar2=None, op0=ALU.mult)
                nc.vector.tensor_scalar(out=bet9[:], in0=bet_bf[:], scalar1=D9 * D9, scalar2=None, op0=ALU.mult)
                for e in range(2):
                    nc.vector.tensor_reduce(
                        out=edge[:, e : e + 1],
                        in_=ident[:].rearrange("p (i x) -> p i x", x=4)[:, 31 * e, :],
                        axis=AX.X,
                        op=ALU.add,
                    )
                nc.vector.tensor_scalar(out=fac[:], in0=edge[:], scalar1=D4 / D6 - RHO, scalar2=RHO, op0=ALU.mult, op1=ALU.add)

            def widen(j):
                hw = hwp.tile([P, 4 * K], BF16, name="hw")
                hb = h_bytes_sb[j]
                if j == 0:
                    for cl in range(4):
                        cols = slice(cl * K, (cl + 1) * K)
                        nc.vector.tensor_tensor(
                            out=hw[:, cols], in0=hb[:, cols].bitcast(FP8), in1=sb4[:, 0:K], op=ALU.mult
                        )
                elif j == NB - 1:
                    nc.vector.tensor_tensor(
                        out=hw[:, K : 3 * K], in0=hb[:, K : 3 * K].bitcast(FP8), in1=sb4[:, K : 3 * K], op=ALU.mult
                    )
                    for cl in (0, 3):
                        cols = slice(cl * K, (cl + 1) * K)
                        nc.vector.tensor_tensor(
                            out=hw[:, cols], in0=hb[:, cols].bitcast(FP8), in1=sb4[:, 0:K], op=ALU.mult
                        )
                else:
                    nc.vector.tensor_tensor(out=hw[:], in0=hb[:].bitcast(FP8), in1=sb4[:], op=ALU.mult)
                widened[j] = hw

            def turn_in(j):
                words = widened[j][:].bitcast(F32)
                g = gp.tile([P, 4 * K], BF16, align_bytes=64, name="g")
                gw = g[:].bitcast(F32)
                for tt in range(TB):
                    xt = pt.tile([P, 2, 2, P], F32, name="turned")
                    for h in range(2):
                        cl = 2 * h + (tt if h else 1 - tt)
                        for u in range(2):
                            nc.tensor.transpose(
                                xt[:, h, u, :], words[:, cl * (K // 2) + u : (cl + 1) * (K // 2) : 2], perm[:]
                            )
                    nc.scalar.copy(
                        out=gw.rearrange("p (h t r u) -> p t h r u", h=2, t=TB, u=2)[:, tt, :, :, :],
                        in_=xt[:].rearrange("p h u r -> p h r u"),
                    )
                grouped[j] = g

            def quantise(j):
                cols = slice(j * 4 * P, (j + 1) * 4 * P)
                nc.vector.quantize_mx(out=codes[:, cols].bitcast(FP8X4), scales=hsc[:, cols], in_=grouped[j][:])

            def column_sum(c):
                for lo, hi in ((0, 2 * P), (2 * P, FS * P)):
                    nc.tensor.matmul_mx(
                        out=colsum[:, lo:hi],
                        lhsT=codes[:, c * P : (c + 1) * P].bitcast(FP8X4),
                        lhsT_scale=hsc[:, c * P : (c + 1) * P],
                        rhs=w_codes[:, lo:hi].bitcast(FP8X4),
                        rhs_scale=w_sc[:, lo:hi],
                        start=(c == 0 and lo == 0),
                        stop=(c == COLS - 1 and lo > 0),
                    )

            trip = one.tile([P, NB, 6], F32)
            waiting = {}

            count = [0]

            def new_y():
                count[0] += 1
                if count[0] % 2:
                    y = py.tile([P, 512], F32, name="y")
                else:
                    y = py1.tile([P, 512], F32, name="y1")
                return y

            def multiply_last(j):
                y = new_y()
                mx_features(y, FS, j * 512)
                waiting[j] = y

            def moments(j):
                nc.vector.bn_stats(out=trip[:, j, :], in_=waiting[j][:])

            def square(j, f):
                y = new_y()
                mx_features(y, f, j * 512)
                junk = jp.tile([P, 512], BF16, name="junk")
                nc.scalar.activation(out=junk[:], in_=y[:], func=ACT.Square, accum_out=ssq[:, f, j : j + 1])

            for s in range(NB + 1):
                if s < NB:
                    widen(s)
                    turn_in(s)
                if s == 1:
                    nc.vector.quantize_mx(
                        out=w_codes[:].bitcast(FP8X4), scales=w_sc[:], in_=w_grp[:].rearrange("p n j -> p (n j)")
                    )
                if s >= 1:
                    quantise(s - 1)
                if s >= 2:
                    moments(s - 2)
                if s == 5:
                    small_constants()
                if s >= 1:
                    j = s - 1
                    if j == NB - 1:
                        for cl in range(4):
                            column_sum(j * 4 + cl)
                        multiply_last(j)
                        for f in range(FS):
                            square(j, f)
                    else:
                        square(j, 0)
                        square(j, 1)
                        column_sum(j * 4)
                        column_sum(j * 4 + 1)
                        square(j, 2)
                        column_sum(j * 4 + 2)
                        multiply_last(j)
                        column_sum(j * 4 + 3)

            cs_sb = one.tile([P, FS * P], F32)
            nc.vector.tensor_copy(out=cs_sb[:], in_=colsum[:, 0 : FS * P])
            moments(NB - 1)
            cst = pt.tile([P, FS, P], F32, name="turned")
            for f in range(FS):
                nc.tensor.transpose(cst[:, f, :], cs_sb[:, f * P : (f + 1) * P], ident[:])
            mv = one.tile([P, 2], F32)
            nc.vector.bn_aggr(out=mv[:], in_=trip[:].rearrange("p j k -> p (j k)"))
            sums = one.tile([P, FS], F32)
            nc.vector.tensor_reduce(out=sums[:], in_=cst[:], axis=AX.X, op=ALU.add)
            nmean = one.tile([P, FC], F32)
            nc.vector.tensor_scalar(out=nmean[:, FS:FC], in0=mv[:, 0:1], scalar1=-1.0, scalar2=None, op0=ALU.mult)
            nc.vector.tensor_scalar(out=nmean[:, 0:FS], in0=sums[:], scalar1=-1.0 / NODES, scalar2=None, op0=ALU.mult)
            ve = one.tile([P, FC], F32)
            nc.vector.tensor_scalar(out=ve[:, FS:FC], in0=mv[:, 1:2], scalar1=0.0, scalar2=EPS_BN, op0=ALU.max, op1=ALU.add)
            m2 = one.tile([P, FS], F32)
            nc.vector.tensor_tensor(out=m2[:], in0=nmean[:, 0:FS], in1=nmean[:, 0:FS], op=ALU.mult)
            gm = one.tile([P, FC], F32)
            nc.vector.tensor_tensor(out=gm[:], in0=nmean[:], in1=g9[:], op=ALU.mult)
            ssq4 = one.tile([P, FS], F32)
            nc.vector.tensor_reduce(out=ssq4[:], in_=ssq[:, 0:FS, :], axis=AX.X, op=ALU.add)
            var = one.tile([P, FS], F32)
            nc.vector.scalar_tensor_tensor(
                out=var[:], in0=ssq4[:], scalar=1.0 / NODES, in1=m2[:], op0=ALU.mult, op1=ALU.subtract
            )
            nc.vector.tensor_scalar(out=ve[:, 0:FS], in0=var[:], scalar1=0.0, scalar2=EPS_BN, op0=ALU.max, op1=ALU.add)
            rstd = one.tile([P, FC], F32)
            nc.scalar.activation(out=rstd[:], in_=ve[:], func=ACT.Abs_reciprocal_sqrt)
            nc.vector.tensor_tensor(out=a9[:], in0=g9[:], in1=rstd[:], op=ALU.mult)
            ma = one.tile([P, FC], F32)
            nc.vector.tensor_tensor(out=ma[:], in0=gm[:], in1=rstd[:], op=ALU.mult)
            nc.vector.tensor_tensor(out=b9[:], in0=bet9[:], in1=ma[:], op=ALU.add)
            nc.vector.tensor_scalar(out=a6[:], in0=a9[:], scalar1=RHO, scalar2=None, op0=ALU.mult)
            nc.vector.tensor_scalar(out=b6[:], in0=b9[:], scalar1=RHO, scalar2=None, op0=ALU.mult)

        with ExitStack() as p2:
            pe = p2.enter_context(tc.psum_pool(name="pe", bufs=2))
            po = p2.enter_context(tc.psum_pool(name="po", bufs=4))
            tvp = p2.enter_context(tc.tile_pool(name="tvp", bufs=5))
            up = p2.enter_context(tc.tile_pool(name="up", bufs=5))
            bp = p2.enter_context(tc.tile_pool(name="bp", bufs=4))
            pp = p2.enter_context(tc.tile_pool(name="pp", bufs=8))
            obp = p2.enter_context(tc.tile_pool(name="obp", bufs=8))

            zh = z_bufs[NZ]
            u_tiles = {}
            three = {}
            turned = {}
            pair = {}

            def relu(out_ap, in_ap, f, a, b):
                nc.scalar.activation(out=out_ap, in_=in_ap, func=ACT.Relu, bias=b[:, f : f + 1], scale=a[:, f : f + 1])

            def norm_relu(j, f):
                zb = z_bufs[j % NZ]
                if j == 0:
                    y = po.tile([P, NF], F32, name="turned_odd")
                elif j == 1 and f < 2:
                    y = pe.tile([P, NF], F32, name="turned_even")
                else:
                    y = py.tile([P, 512], F32, name="y")
                mx_features(y, f, j * 512)
                src = y[:].rearrange("p (h t s x) -> p t s x h", h=2, t=TB, s=2)
                dst = runs(zb)[:, f, :, :, 4:RS].rearrange("p s t (x h) -> p t s x h", h=2)
                if j == NB - 1:
                    relu(dst[:, 0, :, :, :], src[:, 0, :, :, :], f, a9, b9)
                    relu(dst[:, 1, :, :, :], src[:, 1, :, :, :], f, a6, b6)
                else:
                    relu(dst, src, f, a9, b9)

            def swap_columns(f):
                def first(zb):
                    return runs(zb)[:, f, :, 0, 4:RS].rearrange("p s (x h) -> p s x h", h=2)

                nc.vector.tensor_copy(out=first(zh), in_=first(z_bufs[0])[:, :, :, ::-1])

            def weigh(engine, j, f0, f1):
                zb = zh if j < 0 else z_bufs[j % NZ]
                ends = zb[:, f0:f1, P : P + 4 * RS].rearrange("p f (k x) -> p f k x", x=RS)[:, :, :, 0:4]
                if j == NB - 1:
                    parts = ((ends[:, :, 0::2, :], RHO), (ends[:, :, 1::2, :], RHO * KAPPA))
                else:
                    parts = ((ends, RHO),)
                for cells, weight in parts:
                    if engine is nc.scalar:
                        nc.scalar.activation(out=cells, in_=cells, func=ACT.Copy, scale=weight)
                    else:
                        engine.tensor_scalar(out=cells, in0=cells, scalar1=weight, scalar2=0.0, op0=ALU.mult, op1=ALU.add)

            def two_rows(engine, j, f0, f1):
                if j not in u_tiles:
                    u = up.tile([P, FC, TB, P], F32, name="u")
                    u_tiles[j] = u
                zb = zh if j < 0 else z_bufs[j % NZ]
                n = 1 if j < 0 else TB
                engine.tensor_tensor(
                    out=u_tiles[j][:, f0:f1, 0:n, :],
                    in0=runs(zb)[:, f0:f1, 1, 0:n, 4:RS],
                    in1=runs(zb)[:, f0:f1, 0, 0:n, 4:RS],
                    op=ALU.add,
                )

            def border_rows(j):
                zb = zh if j < 0 else z_bufs[j % NZ]
                n = 1 if j < 0 else TB
                for at, lo in ((0, 0), (EV + RS, P - 4)):
                    nc.vector.tensor_scalar(
                        out=zb[:, :, at : at + TB * RS].rearrange("p f (t x) -> p f t x", x=RS)[:, :, 0:n, 0:4],
                        in0=u_tiles[j][:, :, 0:n, lo : lo + 4],
                        scalar1=RHO - 1.0,
                        scalar2=None,
                        op0=ALU.mult,
                    )

            def three_rows(engine, j):
                zb = zh if j < 0 else z_bufs[j % NZ]
                n = 1 if j < 0 else TB
                tv = tvp.tile([P, 2, TB, P], F32, name="tv")
                three[j] = tv
                engine.tensor_tensor(
                    out=tv[:, :, 0:n, :],
                    in0=u_tiles[j][:, 0, 0:n, :].unsqueeze(1).to_broadcast([P, 2, n, P]),
                    in1=windows(zb, n),
                    op=ALU.add,
                )

            def windows(zb, n):
                return zb[:, 0, 0 : 2 * (EV + 8)].rearrange("p (s y) -> p s y", s=2)[:, :, 0 : TB * RS].rearrange(
                    "p s (t x) -> p s t x", x=RS
                )[:, :, 0:n, 0:P]

            def turn_out(t, e):
                j = -1 if t < 0 else t // TB
                tt = 0 if t < 0 else t % TB
                zb = zh if t < 0 else z_bufs[j % NZ]
                if t < 0:
                    o = py.tile([P, NF], F32, name="y")
                elif t % 2 == 0:
                    o = pe.tile([P, NF], F32, name="turned_even")
                else:
                    o = po.tile([P, NF], F32, name="turned_odd")
                w0 = (EV + 8 if e else 0) + tt * RS
                f0 = 1 if j in three else 0
                wins = [(f, u_tiles[j][:, f, tt, :]) for f in range(f0, FC)]
                if j in three:
                    wins.append((0, three[j][:, e, tt, :]))
                wins.extend((f, zb[:, f, w0 : w0 + P]) for f in range(f0, FC))
                for w, (f, win) in enumerate(wins):
                    nc.tensor.matmul(
                        out=o[:, f * P : (f + 1) * P],
                        lhsT=win,
                        rhs=ident[:],
                        is_transpose=True,
                        start=(w == 0),
                        stop=(w == len(wins) - 1),
                    )
                turned[t, e] = o

            def add_turned(dst, t, e, other):
                nc.vector.tensor_tensor(out=dst, in0=turned[t, e][:], in1=other, op=ALU.add)

            out_v = out.rearrange("b (i e c) f -> b c i e f", e=2, c=COLS)
            out_c = out.rearrange("b (i e c) f -> b i e (c f)", e=2, c=COLS)

            def store(ob, k0, t, n):
                for b in range(BATCH):
                    for k in range(n):
                        nc.sync.dma_start(out=out_v[b, 31 - t - k], in_=ob[2 * b : P : 4, :, k0 + k, :])
                    nc.sync.dma_start(
                        out=out_c[b, :, :, (32 + t) * NF : (32 + t + n) * NF],
                        in_=ob[2 * b + 1 : P : 4, :, k0 : k0 + n, :].rearrange("p e k f -> p e (k f)"),
                    )

            for f in range(FC):
                norm_relu(0, f)
                weigh(nc.vector, 0, f, f + 1)
                if f > 0:
                    two_rows(nc.vector, 0, f - 1, f)
            two_rows(nc.vector, 0, FC - 1, FC)
            border_rows(0)
            for f in range(FC):
                swap_columns(f)
            two_rows(nc.vector, -1, 0, FC)
            border_rows(-1)
            pairs = [(j, a) for j in range(1, NB) for a in range(2)]
            done = [0]

            def relus_up_to(n):
                while done[0] < min(n, len(pairs)):
                    j, a = pairs[done[0]]
                    norm_relu(j, 2 * a)
                    norm_relu(j, 2 * a + 1)
                    if a == 1 and j > 1:
                        weigh(nc.scalar, j, 0, FC)
                    done[0] += 1

            for q in range(NB):
                ob = obp.tile([P, 2, TB, NF], F32, name="ob")
                before = [2]
                between = [3]
                relus_up_to(before[q] if q < len(before) else 2 * q + 3)
                if q + 1 < NB:
                    adder = nc.vector if q == 0 else nc.gpsimd
                    for f0 in (0, 2) if q + 1 == NB - 1 else (0,):
                        f1 = f0 + 2 if q + 1 == NB - 1 else FC
                        if q == 0:
                            weigh(nc.vector, 1, 0, FC)
                        two_rows(adder, q + 1, f0, f1)
                if q == 0:
                    idle = po.tile([P, NF], F32, name="turned_odd")
                    for f in range(6):
                        mx_features(idle, f % FC, 0)
                for e in range(2):
                    turn_out(TB * q, e)
                both = {}
                for e in range(2):
                    bt = bp.tile([P, NF], F32, name="bt")
                    nc.scalar.copy(out=bt[:], in_=turned[TB * q, e][:])
                    both[e] = bt
                if q > 0:
                    for e in range(2):
                        add_turned(ob[:, e, 0, :], TB * q, e, pair[q - 1, e][:])
                if q == NB - 1:
                    store(ob, 0, TB * q - 1, 1)
                relus_up_to(between[q] if q < len(between) else 2 * q + 4)
                for e in range(2):
                    turn_out(TB * q + 1, e)
                if q == 1:
                    for e in range(2):
                        turn_out(-1, e)
                if q + 1 < NB:
                    border_rows(q + 1)
                    if 0 < q < NB - 2 - 1:
                        three_rows(nc.vector, q + 1)
                for e in range(2):
                    pr = pp.tile([P, NF], F32, name="pr")
                    add_turned(pr[:], TB * q + 1, e, both[e][:])
                    pair[q, e] = pr
                if q == NB - 1:
                    last = obp.tile([P, 2, TB, NF], F32, name="ob")
                    for e in range(2):
                        nc.scalar.activation(out=last[:, e, 0, :], in_=pair[q, e][:], func=ACT.Copy, scale=fac[:, e : e + 1])
                if q == NB - 1:
                    ob = obp.tile([P, 2, TB, NF], F32, name="ob")
                if q > 0:
                    for e in range(2):
                        add_turned(ob[:, e, 1, :], TB * q - 1, e, pair[q, e][:])
                if q == 1:
                    first = obp.tile([P, 2, TB, NF], F32, name="ob")
                    for e in range(2):
                        add_turned(first[:, e, 0, :], -1, e, pair[0, e][:])
                    store(first, 0, 0, 1)
                if q == NB - 1:
                    store(ob, 1, TB * q, 1)
                    store(last, 0, NT - 1, 1)
                elif q > 0:
                    store(ob, 0, TB * q - 1, TB)
